import numpy as np
import ml_dtypes


def mxq(x, axis, fmt="e4m3"):
    dtype, down = {"e4m3": (ml_dtypes.float8_e4m3fn, 7), "e5m2": (ml_dtypes.float8_e5m2, 14)}[fmt]
    v = np.moveaxis(np.asarray(x, np.float32).astype(ml_dtypes.bfloat16).astype(np.float64), axis, -1)
    blocks = v.reshape(v.shape[:-1] + (-1, 32))
    amax = np.abs(blocks).max(-1, keepdims=True)
    byte = np.maximum(np.where(amax > 0, np.frexp(amax)[1] - 1 + 127, 0) - down, 1)
    scale = np.exp2(byte - 127.0)
    codes = (blocks / scale).astype(np.float32).astype(dtype).astype(np.float64)
    return np.moveaxis((codes * scale).reshape(v.shape), -1, axis)


WIDE = False


def mx_kscale(k):
    if not WIDE:
        return np.ones(k)
    levels = np.array([10, -10, 5, -5, 0])
    a = np.random.permutation(np.resize(levels, k // 512 * 4)).reshape(k // 512, 4)
    idx = np.arange(k)
    return np.exp2(a[idx // 512, idx % 128 // 32])


BF16 = ml_dtypes.bfloat16


def bf(x):
    return np.asarray(x, np.float32).astype(BF16)


def f64(x):
    return np.asarray(x).astype(np.float64)


B, H, W, FI, FO = 4, 32, 32, 512, 1024

OFFSETS = [(-1, 0), (1, 0), (0, -1), (0, 1), (-1, -1), (-1, 1), (1, -1), (1, 1)]


def setup_inputs():
    s = mx_kscale(FI)
    return {"X": bf(np.random.standard_normal((B, H * W, FI)) * 0.5 * s),
            "Wm": bf(np.random.standard_normal((FI, FO)) / np.sqrt(FI) / s[:, None]),
            "b": bf(np.random.standard_normal(FO) * 0.2),
            "H": H, "W": W}


def reference(X, Wm, b, H, W):
    X = f64(X)
    Bn, N, F = X.shape
    Xg = X.reshape(Bn, H, W, F)
    P = np.pad(Xg, ((0, 0), (1, 1), (1, 1), (0, 0)))
    AX = P[:, 1 + OFFSETS[0][0]:1 + OFFSETS[0][0] + H,
           1 + OFFSETS[0][1]:1 + OFFSETS[0][1] + W, :]
    for dr, dc in OFFSETS[1:]:
        AX = AX + P[:, 1 + dr:1 + dr + H, 1 + dc:1 + dc + W, :]
    AX = AX.reshape(Bn, N, F)
    return (mxq(AX, 2, "e4m3") @ mxq(f64(Wm), 0, "e4m3")) + f64(b)

@@ -1,0 +1,197 @@
+from contextlib import ExitStack
+
+import concourse.mybir as mybir
+from concourse.masks import make_identity
+
+BF16 = mybir.dt.bfloat16
+F32 = mybir.dt.float32
+U32 = mybir.dt.uint32
+U8 = mybir.dt.uint8
+FP8X4 = mybir.dt.float8_e4m3fn_x4
+ADD = mybir.AluOpType.add
+
+P = 128
+FLOPS = 2 * 4096 * 512 * 1024
+
+G_OUT_EVERY = 4
+G_TS_EVERY = 2
+
+
+def tile_graphconvlayer_kernel(tc, X, Wm, b, H, W, out):
+    nc = tc.nc
+    n_feat = X.shape[2]
+    n_out = Wm.shape[1]
+    n_t = n_feat // P
+
+    xp_view = X[0:2].rearrange("b (j p) f -> p (b j) f", p=P)
+    op_view = out[0:2].rearrange("b (j p) n -> p (b j) n", p=P)
+    xz_flat = X[2:4].rearrange("b n f -> (b n) f")
+    xz_view = xz_flat.rearrange("(p i) f -> p i f", i=16)
+    xz_rows = xz_flat.rearrange("(m k) f -> m k f", k=32)
+    oz_view = out[2:4].rearrange("b n f -> (b n) f").rearrange("(p i) n -> p i n", i=16)
+
+    with ExitStack() as ctx:
+        const = ctx.enter_context(tc.tile_pool(name="const", bufs=1))
+        ts_pool = ctx.enter_context(tc.tile_pool(name="ts", bufs=4))
+        work = ctx.enter_context(tc.tile_pool(name="work", bufs=4))
+        stage = ctx.enter_context(tc.tile_pool(name="stage", bufs=6))
+        ps_a = ctx.enter_context(tc.psum_pool(name="ps_a", bufs=3))
+        ps_o = ctx.enter_context(tc.psum_pool(name="ps_o", bufs=5))
+
+        xs = const.tile([P, 16, n_feat], BF16)
+        xz = const.tile([P, 18, n_feat], BF16)
+        xf = const.tile([P, 2, 2, n_feat], BF16)
+        w_raw = const.tile([P, n_t, n_out], BF16)
+        b_bc = const.tile([P, n_out], BF16)
+        eye = const.tile([P, 260], BF16)
+        id32 = const.tile([P, P], F32)
+
+        nc.vector.memset(eye[:], 0.0)
+        nc.vector.memset(id32[:], 0.0)
+        nc.vector.memset(xz[:, 0, :], 0.0)
+        nc.vector.memset(xz[:, 17, :], 0.0)
+
+        w_view = Wm.rearrange("(t p) n -> p t n", p=P)
+        nc.scalar.dma_start(out=b_bc[:], in_=b.partition_broadcast(P))
+        nc.sync.dma_start(out=w_raw[:, :, 0:512], in_=w_view[:, :, 0:512])
+        nc.sync.dma_start(out=xs[:, 0:2, :], in_=xp_view[:, 0:2, :])
+        nc.sync.dma_start(out=w_raw[:, :, 512:1024], in_=w_view[:, :, 512:1024])
+        nc.sync.dma_start(out=xz[1:128:2, 0, :], in_=xz_rows[:, 15, :])
+        nc.sync.dma_start(out=xz[:, 1:5, :], in_=xz_view[:, 0:4, :])
+        nc.sync.dma_start(out=xs[:, 2:4, :], in_=xp_view[:, 2:4, :])
+        nc.sync.dma_start(out=xf[:, 0, :, :], in_=X[2:4, 0:128, :].rearrange("b p f -> p b f"))
+        nc.sync.dma_start(out=xf[:, 1, :, :], in_=X[2:4, 896:1024, :].rearrange("b p f -> p b f"))
+        nc.sync.dma_start(out=xs[:, 4:8, :], in_=xp_view[:, 4:8, :])
+        nc.sync.dma_start(out=xz[:, 5:9, :], in_=xz_view[:, 4:8, :])
+        nc.sync.dma_start(out=xs[:, 8:12, :], in_=xp_view[:, 8:12, :])
+        nc.sync.dma_start(out=xz[:, 9:13, :], in_=xz_view[:, 8:12, :])
+        nc.sync.dma_start(out=xs[:, 12:16, :], in_=xp_view[:, 12:16, :])
+        nc.sync.dma_start(out=xz[:, 13:17, :], in_=xz_view[:, 12:16, :])
+        nc.sync.dma_start(out=xz[0:128:2, 17, :], in_=xz_rows[:, 16, :])
+
+        make_identity(nc, eye[:, 66:194], nomemset=True)
+        make_identity(nc, id32[:], nomemset=True)
+        r2 = const.tile([P, 194], BF16)
+        r3 = const.tile([P, 194], BF16)
+        a1 = const.tile([P, 192], BF16)
+        adj = const.tile([P, 192], BF16)
+        nc.vector.tensor_tensor(out=r2[:], in0=eye[:, 1:195], in1=eye[:, 65:259], op=ADD)
+        nc.vector.tensor_tensor(out=r3[:], in0=r2[:], in1=eye[:, 33:227], op=ADD)
+        nc.vector.tensor_tensor(out=a1[:], in0=r2[:, 1:193], in1=r3[:, 0:192], op=ADD)
+        nc.vector.tensor_copy(
+            out=a1[:].rearrange("p (r c) -> p r c", c=32)[:, :, 0:1],
+            in_=r2[:, 1:193].rearrange("p (r c) -> p r c", c=32)[:, :, 0:1],
+        )
+        nc.vector.tensor_tensor(out=adj[:], in0=a1[:], in1=r3[:, 2:194], op=ADD)
+        nc.vector.tensor_copy(
+            out=adj[:].rearrange("p (r c) -> p r c", c=32)[:, :, 31:32],
+            in_=a1[:].rearrange("p (r c) -> p r c", c=32)[:, :, 31:32],
+        )
+        cyc_up = const.tile([P, P], F32)
+        cyc_dn = const.tile([P, P], F32)
+        nc.vector.tensor_copy(out=cyc_up[:, 2:128], in_=id32[:, 0:126])
+        nc.vector.tensor_copy(out=cyc_up[:, 0:2], in_=id32[:, 126:128])
+        nc.vector.tensor_copy(out=cyc_dn[:, 0:126], in_=id32[:, 2:128])
+        nc.vector.tensor_copy(out=cyc_dn[:, 126:128], in_=id32[:, 0:2])
+
+        w_grp = const.tile([P, n_out, n_t], BF16, align_bytes=64)
+        w_q = const.tile([P, n_out], U32, align_bytes=64)
+        w_s = const.tile([P, n_out], U8, align_bytes=64)
+        nc.vector.tensor_copy(out=w_grp[:, 0:512, :], in_=w_raw[:, :, 0:512].rearrange("p t n -> p n t"))
+        nc.scalar.copy(out=w_grp[:, 512:1024, :], in_=w_raw[:, :, 512:1024].rearrange("p t n -> p n t"))
+        for h in range(2):
+            cols = slice(512 * h, 512 * h + 512)
+            nc.vector.quantize_mx(out=w_q[:, cols].bitcast(FP8X4), scales=w_s[:, cols],
+                                  in_=w_grp[:, cols, :].rearrange("p n t -> p (n t)"))
+        bias = const.tile([P, n_out], F32)
+        nc.scalar.copy(out=bias[:], in_=b_bc[:])
+
+        fix = const.tile([P, 16, 4, 2, n_t], BF16)
+
+        def border_rows():
+            acc_f = ps_a.tile([P, n_t, P], F32, tag="acc")
+            for t in range(n_t):
+                f = slice(P * t, P * t + P)
+                for q in range(4):
+                    rr = q % 2
+                    a_cols = slice(32, 64) if rr == 0 else slice(128, 160)
+                    nc.tensor.matmul(acc_f[:, t, 32 * q:32 * q + 32], lhsT=xf[:, rr, q // 2, f], rhs=adj[:, a_cols],
+                                     start=True, stop=True)
+            for q in range(4):
+                nc.scalar.copy(out=fix[:, :, q, :, :],
+                               in_=acc_f[:, :, 32 * q:32 * q + 32].rearrange("p t (h i) -> p i h t", h=2))
+
+        counter = [0]
+
+        def finish(acc, dest, patch):
+            grp = work.tile([P, P, n_t], BF16, align_bytes=64, tag="grp")
+            nc.scalar.copy(out=grp[:], in_=acc[:].rearrange("p t n -> p n t"))
+            if patch is not None:
+                dst = grp[:].rearrange("p (b x) t -> p b (x t)", b=2)
+                src = fix[:, patch, :, :, :].rearrange("p (b r) h t -> p b r (h t)", b=2)
+                nc.scalar.copy(out=dst[:, :, 0:8], in_=src[:, :, 0, :])
+                nc.scalar.copy(out=dst[:, :, 248:256], in_=src[:, :, 1, :])
+            a_q = work.tile([P, P], U32, align_bytes=64, tag="a_q")
+            a_s = work.tile([P, P], U8, align_bytes=64, tag="a_s")
+            nc.vector.quantize_mx(out=a_q[:].bitcast(FP8X4), scales=a_s[:],
+                                  in_=grp[:].rearrange("p n t -> p (n t)"))
+            o_sb = stage.tile([P, n_out], F32, tag="o_sb")
+            for h in range(2):
+                cols = slice(512 * h, 512 * h + 512)
+                po = ps_o.tile([P, 512], F32, tag="po")
+                nc.tensor.matmul_mx(out=po[:], lhsT=a_q[:].bitcast(FP8X4), lhsT_scale=a_s[:],
+                                    rhs=w_q[:, cols].bitcast(FP8X4), rhs_scale=w_s[:, cols],
+                                    start=True, stop=True)
+                counter[0] += 1
+                if counter[0] % G_OUT_EVERY == 0:
+                    nc.scalar.copy(out=o_sb[:, cols], in_=po[:])
+                    nc.gpsimd.tensor_tensor(out=o_sb[:, cols], in0=o_sb[:, cols], in1=bias[:, cols], op=ADD)
+                else:
+                    nc.vector.tensor_tensor(out=o_sb[:, cols], in0=po[:], in1=bias[:, cols], op=ADD)
+            nc.sync.dma_start(out=dest, in_=o_sb[:])
+
+        def p_block(g):
+            j = g % 8
+            has_up = j > 0
+            has_dn = j < 7
+            acc = ps_a.tile([P, n_t, P], F32, tag="acc")
+            for t in range(n_t):
+                f = slice(P * t, P * t + P)
+                nc.tensor.matmul(acc[:, t, :], lhsT=xs[:, g, f], rhs=adj[:, 32:160],
+                                 start=True, stop=not (has_up or has_dn))
+                if has_up:
+                    nc.tensor.matmul(acc[:, t, 0:32], lhsT=xs[:, g - 1, f], rhs=adj[:, 160:192],
+                                     start=False, stop=not has_dn)
+                if has_dn:
+                    nc.tensor.matmul(acc[:, t, 96:128], lhsT=xs[:, g + 1, f], rhs=adj[:, 0:32],
+                                     start=False, stop=True)
+            return acc
+
+        def z_sums(ci):
+            eng = nc.gpsimd if ci % G_TS_EVERY == 1 else nc.vector
+            t32 = ts_pool.tile([P, n_feat], F32, tag="t32")
+            s32 = ts_pool.tile([P, n_feat], F32, tag="s32")
+            eng.tensor_tensor(out=t32[:], in0=xz[:, ci, :], in1=xz[:, ci + 2, :], op=ADD)
+            eng.tensor_tensor(out=s32[:], in0=t32[:], in1=xz[:, ci + 1, :], op=ADD)
+            return t32, s32
+
+        def z_block(t32, s32):
+            acc = ps_a.tile([P, n_t, P], F32, tag="acc")
+            for t in range(n_t):
+                f = slice(P * t, P * t + P)
+                nc.tensor.matmul(acc[:, t, :], lhsT=t32[:, f], rhs=id32[:],
+                                 is_transpose=True, start=True, stop=False)
+                nc.tensor.matmul(acc[:, t, :], lhsT=s32[:, f], rhs=cyc_up[:],
+                                 is_transpose=True, start=False, stop=False)
+                nc.tensor.matmul(acc[:, t, :], lhsT=s32[:, f], rhs=cyc_dn[:],
+                                 is_transpose=True, start=False, stop=True)
+            return acc
+
+        for i in range(16):
+            sums = z_sums(i)
+            acc_p = p_block(i)
+            finish(acc_p, op_view[:, i, :], None)
+            if i == 0:
+                border_rows()
+            acc_z = z_block(sums[0], sums[1])
+            finish(acc_z, oz_view[:, i, :], i)

@@ -13,8 +13,8 @@ ADD = mybir.AluOpType.add
 P = 128
 FLOPS = 2 * 4096 * 512 * 1024
 
-G_OUT_EVERY = 4
-G_TS_EVERY = 2
+G_OUT_EVERY = 1000
+G_TS_EVERY = 1000
 
 
 def tile_graphconvlayer_kernel(tc, X, Wm, b, H, W, out):

@@ -13,8 +13,8 @@ ADD = mybir.AluOpType.add
 P = 128
 FLOPS = 2 * 4096 * 512 * 1024
 
-G_OUT_EVERY = 1000
-G_TS_EVERY = 1000
+S2_QUADS = (0, 1, 2)
+V_COPY_EVERY = 1000
 
 
 def tile_graphconvlayer_kernel(tc, X, Wm, b, H, W, out):
@@ -34,7 +34,9 @@ def tile_graphconvlayer_kernel(tc, X, Wm, b, H, W, out):
         const = ctx.enter_context(tc.tile_pool(name="const", bufs=1))
         ts_pool = ctx.enter_context(tc.tile_pool(name="ts", bufs=4))
         work = ctx.enter_context(tc.tile_pool(name="work", bufs=4))
-        stage = ctx.enter_context(tc.tile_pool(name="stage", bufs=6))
+        quad = ctx.enter_context(tc.tile_pool(name="quad", bufs=2))
+        back = ctx.enter_context(tc.tile_pool(name="back", bufs=8))
+        stage = ctx.enter_context(tc.tile_pool(name="stage", bufs=8))
         ps_a = ctx.enter_context(tc.psum_pool(name="ps_a", bufs=3))
         ps_o = ctx.enter_context(tc.psum_pool(name="ps_o", bufs=5))
 
@@ -43,19 +45,35 @@ def tile_graphconvlayer_kernel(tc, X, Wm, b, H, W, out):
         xf = const.tile([P, 2, 2, n_feat], BF16)
         w_raw = const.tile([P, n_t, n_out], BF16)
         b_bc = const.tile([P, n_out], BF16)
+        b_rows = const.tile([P, P], BF16)
         eye = const.tile([P, 260], BF16)
         id32 = const.tile([P, P], F32)
-
-        nc.vector.memset(eye[:], 0.0)
-        nc.vector.memset(id32[:], 0.0)
-        nc.vector.memset(xz[:, 0, :], 0.0)
-        nc.vector.memset(xz[:, 17, :], 0.0)
+        idx = const.tile([P, 260], F32, align_bytes=64)
+        low = const.tile([P, 32], F32, align_bytes=64)
+        pos = const.tile([P, 1], F32)
 
         w_view = Wm.rearrange("(t p) n -> p t n", p=P)
+        nc.vector.memset(b_rows[:], 0.0)
+        nc.scalar.dma_start(out=b_rows[0:8, :], in_=b.rearrange("(m p) -> m p", p=P))
         nc.scalar.dma_start(out=b_bc[:], in_=b.partition_broadcast(P))
         nc.sync.dma_start(out=w_raw[:, :, 0:512], in_=w_view[:, :, 0:512])
         nc.sync.dma_start(out=xs[:, 0:2, :], in_=xp_view[:, 0:2, :])
         nc.sync.dma_start(out=w_raw[:, :, 512:1024], in_=w_view[:, :, 512:1024])
+
+        nc.vector.memset(idx[:, 0:1], 0.0)
+        for w in (1, 2, 4, 8, 16, 32, 64, 128, 256):
+            n = min(w, 260 - w)
+            nc.vector.tensor_scalar_add(out=idx[:, w:w + n], in0=idx[:, 0:n], scalar1=float(w))
+        nc.vector.transpose(out=low[:], in_=idx[:, 0:32])
+        for q in range(4):
+            rows = slice(32 * q, 32 * q + 32)
+            nc.vector.tensor_scalar_add(out=pos[rows, :], in0=low[rows, 0:1], scalar1=float(32 * q + 66))
+        nc.vector.tensor_scalar(out=eye[:], in0=idx[:], scalar1=pos[:, 0:1], scalar2=None,
+                                op0=mybir.AluOpType.is_equal)
+        nc.vector.tensor_copy(out=id32[:], in_=eye[:, 66:194])
+
+        nc.vector.memset(xz[:, 0, :], 0.0)
+        nc.vector.memset(xz[:, 17, :], 0.0)
         nc.sync.dma_start(out=xz[1:128:2, 0, :], in_=xz_rows[:, 15, :])
         nc.sync.dma_start(out=xz[:, 1:5, :], in_=xz_view[:, 0:4, :])
         nc.sync.dma_start(out=xs[:, 2:4, :], in_=xp_view[:, 2:4, :])
@@ -69,8 +87,6 @@ def tile_graphconvlayer_kernel(tc, X, Wm, b, H, W, out):
         nc.sync.dma_start(out=xz[:, 13:17, :], in_=xz_view[:, 12:16, :])
         nc.sync.dma_start(out=xz[0:128:2, 17, :], in_=xz_rows[:, 16, :])
 
-        make_identity(nc, eye[:, 66:194], nomemset=True)
-        make_identity(nc, id32[:], nomemset=True)
         r2 = const.tile([P, 194], BF16)
         r3 = const.tile([P, 194], BF16)
         a1 = const.tile([P, 192], BF16)
@@ -105,6 +121,10 @@ def tile_graphconvlayer_kernel(tc, X, Wm, b, H, W, out):
                                   in_=w_grp[:, cols, :].rearrange("p n t -> p (n t)"))
         bias = const.tile([P, n_out], F32)
         nc.scalar.copy(out=bias[:], in_=b_bc[:])
+        b_col = const.tile([P, 8], F32)
+        pbt = ps_o.tile([P, P], BF16, tag="po")
+        nc.tensor.transpose(out=pbt[:], in_=b_rows[:], identity=eye[:, 66:194])
+        nc.vector.tensor_copy(out=b_col[:], in_=pbt[:, 0:8])
 
         fix = const.tile([P, 16, 4, 2, n_t], BF16)
 
@@ -121,9 +141,7 @@ def tile_graphconvlayer_kernel(tc, X, Wm, b, H, W, out):
                 nc.scalar.copy(out=fix[:, :, q, :, :],
                                in_=acc_f[:, :, 32 * q:32 * q + 32].rearrange("p t (h i) -> p i h t", h=2))
 
-        counter = [0]
-
-        def finish(acc, dest, patch):
+        def quantise(acc, patch, a_q, a_s):
             grp = work.tile([P, P, n_t], BF16, align_bytes=64, tag="grp")
             nc.scalar.copy(out=grp[:], in_=acc[:].rearrange("p t n -> p n t"))
             if patch is not None:
@@ -131,24 +149,50 @@ def tile_graphconvlayer_kernel(tc, X, Wm, b, H, W, out):
                 src = fix[:, patch, :, :, :].rearrange("p (b r) h t -> p b r (h t)", b=2)
                 nc.scalar.copy(out=dst[:, :, 0:8], in_=src[:, :, 0, :])
                 nc.scalar.copy(out=dst[:, :, 248:256], in_=src[:, :, 1, :])
-            a_q = work.tile([P, P], U32, align_bytes=64, tag="a_q")
-            a_s = work.tile([P, P], U8, align_bytes=64, tag="a_s")
-            nc.vector.quantize_mx(out=a_q[:].bitcast(FP8X4), scales=a_s[:],
-                                  in_=grp[:].rearrange("p n t -> p (n t)"))
+            nc.vector.quantize_mx(out=a_q.bitcast(FP8X4), scales=a_s, in_=grp[:].rearrange("p n t -> p (n t)"))
+
+        def direct_out(a_q, a_s, dest):
             o_sb = stage.tile([P, n_out], F32, tag="o_sb")
             for h in range(2):
                 cols = slice(512 * h, 512 * h + 512)
                 po = ps_o.tile([P, 512], F32, tag="po")
-                nc.tensor.matmul_mx(out=po[:], lhsT=a_q[:].bitcast(FP8X4), lhsT_scale=a_s[:],
+                nc.tensor.matmul_mx(out=po[:], lhsT=a_q.bitcast(FP8X4), lhsT_scale=a_s,
                                     rhs=w_q[:, cols].bitcast(FP8X4), rhs_scale=w_s[:, cols],
                                     start=True, stop=True)
-                counter[0] += 1
-                if counter[0] % G_OUT_EVERY == 0:
-                    nc.scalar.copy(out=o_sb[:, cols], in_=po[:])
-                    nc.gpsimd.tensor_tensor(out=o_sb[:, cols], in0=o_sb[:, cols], in1=bias[:, cols], op=ADD)
-                else:
-                    nc.vector.tensor_tensor(out=o_sb[:, cols], in0=po[:], in1=bias[:, cols], op=ADD)
+                nc.vector.tensor_tensor(out=o_sb[:, cols], in0=po[:], in1=bias[:, cols], op=ADD)
             nc.sync.dma_start(out=dest, in_=o_sb[:])
+
+        copies = [0]
+
+        def transposed_out(a_q4, a_s4, dests):
+            o_tiles = []
+            for u in range(4):
+                o_u = stage.tile([P, n_out], F32, tag="o_sb", name="o_u%d" % u)
+                o_tiles.append(o_u)
+            for h in range(2):
+                o_t = []
+                for q in range(4):
+                    m = 4 * h + q
+                    cols = slice(P * m, P * m + P)
+                    po = ps_o.tile([P, 512], F32, tag="po")
+                    nc.tensor.matmul_mx(out=po[:], lhsT=w_q[:, cols].bitcast(FP8X4), lhsT_scale=w_s[:, cols],
+                                        rhs=a_q4[:].bitcast(FP8X4), rhs_scale=a_s4[:], start=True, stop=True)
+                    o_m = back.tile([P, 512], F32, tag="o_m", name="o_m%d" % q)
+                    nc.scalar.activation(out=o_m[:], in_=po[:], func=mybir.ActivationFunctionType.Identity,
+                                         bias=b_col[:, m:m + 1], scale=1.0)
+                    o_t.append(o_m)
+                for u in range(4):
+                    pt = ps_o.tile([P, 512], F32, tag="po")
+                    for q in range(4):
+                        nc.tensor.transpose(out=pt[:, P * q:P * q + P], in_=o_t[q][:, P * u:P * u + P],
+                                            identity=id32[:])
+                    copies[0] += 1
+                    if copies[0] % V_COPY_EVERY == 0:
+                        nc.vector.tensor_copy(out=o_tiles[u][:, 512 * h:512 * h + 512], in_=pt[:])
+                    else:
+                        nc.scalar.copy(out=o_tiles[u][:, 512 * h:512 * h + 512], in_=pt[:])
+            for u in range(4):
+                nc.sync.dma_start(out=dests[u], in_=o_tiles[u][:])
 
         def p_block(g):
             j = g % 8
@@ -168,11 +212,10 @@ def tile_graphconvlayer_kernel(tc, X, Wm, b, H, W, out):
             return acc
 
         def z_sums(ci):
-            eng = nc.gpsimd if ci % G_TS_EVERY == 1 else nc.vector
             t32 = ts_pool.tile([P, n_feat], F32, tag="t32")
             s32 = ts_pool.tile([P, n_feat], F32, tag="s32")
-            eng.tensor_tensor(out=t32[:], in0=xz[:, ci, :], in1=xz[:, ci + 2, :], op=ADD)
-            eng.tensor_tensor(out=s32[:], in0=t32[:], in1=xz[:, ci + 1, :], op=ADD)
+            nc.vector.tensor_tensor(out=t32[:], in0=xz[:, ci, :], in1=xz[:, ci + 2, :], op=ADD)
+            nc.vector.tensor_tensor(out=s32[:], in0=t32[:], in1=xz[:, ci + 1, :], op=ADD)
             return t32, s32
 
         def z_block(t32, s32):
@@ -187,11 +230,21 @@ def tile_graphconvlayer_kernel(tc, X, Wm, b, H, W, out):
                                  is_transpose=True, start=False, stop=True)
             return acc
 
-        for i in range(16):
-            sums = z_sums(i)
-            acc_p = p_block(i)
-            finish(acc_p, op_view[:, i, :], None)
-            if i == 0:
-                border_rows()
-            acc_z = z_block(sums[0], sums[1])
-            finish(acc_z, oz_view[:, i, :], i)
+        for k in range(4):
+            a_q4 = quad.tile([P, 512], U32, align_bytes=64, tag="a_q4")
+            a_s4 = quad.tile([P, 512], U8, align_bytes=64, tag="a_s4")
+            for u in range(4):
+                i = 4 * k + u
+                sums = z_sums(i)
+                a_q = work.tile([P, P], U32, align_bytes=64, tag="a_q")
+                a_s = work.tile([P, P], U8, align_bytes=64, tag="a_s")
+                quantise(p_block(i), None, a_q[:], a_s[:])
+                direct_out(a_q[:], a_s[:], op_view[:, i, :])
+                if i == 0:
+                    border_rows()
+                cols = slice(P * u, P * u + P)
+                quantise(z_block(sums[0], sums[1]), i, a_q4[:, cols], a_s4[:, cols])
+                if k not in S2_QUADS:
+                    direct_out(a_q4[:, cols], a_s4[:, cols], oz_view[:, i, :])
+            if k in S2_QUADS:
+                transposed_out(a_q4, a_s4, [oz_view[:, 4 * k + u, :] for u in range(4)])

@@ -13,8 +13,7 @@ ADD = mybir.AluOpType.add
 P = 128
 FLOPS = 2 * 4096 * 512 * 1024
 
-S2_QUADS = (0, 1, 2)
-V_COPY_EVERY = 1000
+G_HALF = None
 
 
 def tile_graphconvlayer_kernel(tc, X, Wm, b, H, W, out):
@@ -29,36 +28,57 @@ def tile_graphconvlayer_kernel(tc, X, Wm, b, H, W, out):
     xz_view = xz_flat.rearrange("(p i) f -> p i f", i=16)
     xz_rows = xz_flat.rearrange("(m k) f -> m k f", k=32)
     oz_view = out[2:4].rearrange("b n f -> (b n) f").rearrange("(p i) n -> p i n", i=16)
+    w_view = Wm.rearrange("(t p) n -> p t n", p=P)
 
     with ExitStack() as ctx:
         const = ctx.enter_context(tc.tile_pool(name="const", bufs=1))
-        ts_pool = ctx.enter_context(tc.tile_pool(name="ts", bufs=4))
-        work = ctx.enter_context(tc.tile_pool(name="work", bufs=4))
-        quad = ctx.enter_context(tc.tile_pool(name="quad", bufs=2))
-        back = ctx.enter_context(tc.tile_pool(name="back", bufs=8))
-        stage = ctx.enter_context(tc.tile_pool(name="stage", bufs=8))
-        ps_a = ctx.enter_context(tc.psum_pool(name="ps_a", bufs=3))
-        ps_o = ctx.enter_context(tc.psum_pool(name="ps_o", bufs=5))
+        ts_pool = ctx.enter_context(tc.tile_pool(name="ts", bufs=3))
+        work = ctx.enter_context(tc.tile_pool(name="work", bufs=2))
+        stage = ctx.enter_context(tc.tile_pool(name="stage", bufs=6))
+        ps_a = ctx.enter_context(tc.psum_pool(name="ps_a", bufs=2))
+        ps_o = ctx.enter_context(tc.psum_pool(name="ps_o", bufs=4))
+        ctx.enter_context(tc.manual_schedule())
 
         xs = const.tile([P, 16, n_feat], BF16)
         xz = const.tile([P, 18, n_feat], BF16)
         xf = const.tile([P, 2, 2, n_feat], BF16)
         w_raw = const.tile([P, n_t, n_out], BF16)
         b_bc = const.tile([P, n_out], BF16)
-        b_rows = const.tile([P, P], BF16)
         eye = const.tile([P, 260], BF16)
         id32 = const.tile([P, P], F32)
         idx = const.tile([P, 260], F32, align_bytes=64)
         low = const.tile([P, 32], F32, align_bytes=64)
         pos = const.tile([P, 1], F32)
+        r2 = const.tile([P, 194], BF16)
+        r3 = const.tile([P, 194], BF16)
+        a1 = const.tile([P, 192], BF16)
+        adj = const.tile([P, 192], BF16)
+        cyc_up = const.tile([P, P], F32)
+        cyc_dn = const.tile([P, P], F32)
+        w_grp = const.tile([P, n_out, n_t], BF16, align_bytes=64)
+        w_q = const.tile([P, n_out], U32, align_bytes=64)
+        w_s = const.tile([P, n_out], U8, align_bytes=64)
+        bias = const.tile([P, n_out], F32)
+        fix = const.tile([P, 16, 4, 2, n_t], BF16)
 
-        w_view = Wm.rearrange("(t p) n -> p t n", p=P)
-        nc.vector.memset(b_rows[:], 0.0)
-        nc.scalar.dma_start(out=b_rows[0:8, :], in_=b.rearrange("(m p) -> m p", p=P))
+        nc.vector.memset(xz[:, 0, :], 0.0)
+        nc.vector.memset(xz[:, 17, :], 0.0)
         nc.scalar.dma_start(out=b_bc[:], in_=b.partition_broadcast(P))
         nc.sync.dma_start(out=w_raw[:, :, 0:512], in_=w_view[:, :, 0:512])
         nc.sync.dma_start(out=xs[:, 0:2, :], in_=xp_view[:, 0:2, :])
+        nc.sync.dma_start(out=xz[1:128:2, 0, :], in_=xz_rows[:, 15, :])
+        nc.sync.dma_start(out=xz[:, 1:5, :], in_=xz_view[:, 0:4, :])
         nc.sync.dma_start(out=w_raw[:, :, 512:1024], in_=w_view[:, :, 512:1024])
+        nc.sync.dma_start(out=xf[:, 0, :, :], in_=X[2:4, 0:128, :].rearrange("b p f -> p b f"))
+        nc.sync.dma_start(out=xf[:, 1, :, :], in_=X[2:4, 896:1024, :].rearrange("b p f -> p b f"))
+        nc.sync.dma_start(out=xs[:, 2:4, :], in_=xp_view[:, 2:4, :])
+        nc.sync.dma_start(out=xs[:, 4:8, :], in_=xp_view[:, 4:8, :])
+        nc.sync.dma_start(out=xz[:, 5:9, :], in_=xz_view[:, 4:8, :])
+        nc.sync.dma_start(out=xs[:, 8:12, :], in_=xp_view[:, 8:12, :])
+        nc.sync.dma_start(out=xz[:, 9:13, :], in_=xz_view[:, 8:12, :])
+        nc.sync.dma_start(out=xs[:, 12:16, :], in_=xp_view[:, 12:16, :])
+        nc.sync.dma_start(out=xz[:, 13:17, :], in_=xz_view[:, 12:16, :])
+        nc.sync.dma_start(out=xz[0:128:2, 17, :], in_=xz_rows[:, 16, :])
 
         nc.vector.memset(idx[:, 0:1], 0.0)
         for w in (1, 2, 4, 8, 16, 32, 64, 128, 256):
@@ -70,27 +90,6 @@ def tile_graphconvlayer_kernel(tc, X, Wm, b, H, W, out):
             nc.vector.tensor_scalar_add(out=pos[rows, :], in0=low[rows, 0:1], scalar1=float(32 * q + 66))
         nc.vector.tensor_scalar(out=eye[:], in0=idx[:], scalar1=pos[:, 0:1], scalar2=None,
                                 op0=mybir.AluOpType.is_equal)
-        nc.vector.tensor_copy(out=id32[:], in_=eye[:, 66:194])
-
-        nc.vector.memset(xz[:, 0, :], 0.0)
-        nc.vector.memset(xz[:, 17, :], 0.0)
-        nc.sync.dma_start(out=xz[1:128:2, 0, :], in_=xz_rows[:, 15, :])
-        nc.sync.dma_start(out=xz[:, 1:5, :], in_=xz_view[:, 0:4, :])
-        nc.sync.dma_start(out=xs[:, 2:4, :], in_=xp_view[:, 2:4, :])
-        nc.sync.dma_start(out=xf[:, 0, :, :], in_=X[2:4, 0:128, :].rearrange("b p f -> p b f"))
-        nc.sync.dma_start(out=xf[:, 1, :, :], in_=X[2:4, 896:1024, :].rearrange("b p f -> p b f"))
-        nc.sync.dma_start(out=xs[:, 4:8, :], in_=xp_view[:, 4:8, :])
-        nc.sync.dma_start(out=xz[:, 5:9, :], in_=xz_view[:, 4:8, :])
-        nc.sync.dma_start(out=xs[:, 8:12, :], in_=xp_view[:, 8:12, :])
-        nc.sync.dma_start(out=xz[:, 9:13, :], in_=xz_view[:, 8:12, :])
-        nc.sync.dma_start(out=xs[:, 12:16, :], in_=xp_view[:, 12:16, :])
-        nc.sync.dma_start(out=xz[:, 13:17, :], in_=xz_view[:, 12:16, :])
-        nc.sync.dma_start(out=xz[0:128:2, 17, :], in_=xz_rows[:, 16, :])
-
-        r2 = const.tile([P, 194], BF16)
-        r3 = const.tile([P, 194], BF16)
-        a1 = const.tile([P, 192], BF16)
-        adj = const.tile([P, 192], BF16)
         nc.vector.tensor_tensor(out=r2[:], in0=eye[:, 1:195], in1=eye[:, 65:259], op=ADD)
         nc.vector.tensor_tensor(out=r3[:], in0=r2[:], in1=eye[:, 33:227], op=ADD)
         nc.vector.tensor_tensor(out=a1[:], in0=r2[:, 1:193], in1=r3[:, 0:192], op=ADD)
@@ -103,33 +102,23 @@ def tile_graphconvlayer_kernel(tc, X, Wm, b, H, W, out):
             out=adj[:].rearrange("p (r c) -> p r c", c=32)[:, :, 31:32],
             in_=a1[:].rearrange("p (r c) -> p r c", c=32)[:, :, 31:32],
         )
-        cyc_up = const.tile([P, P], F32)
-        cyc_dn = const.tile([P, P], F32)
+        nc.vector.tensor_copy(out=id32[:], in_=eye[:, 66:194])
         nc.vector.tensor_copy(out=cyc_up[:, 2:128], in_=id32[:, 0:126])
         nc.vector.tensor_copy(out=cyc_up[:, 0:2], in_=id32[:, 126:128])
         nc.vector.tensor_copy(out=cyc_dn[:, 0:126], in_=id32[:, 2:128])
         nc.vector.tensor_copy(out=cyc_dn[:, 126:128], in_=id32[:, 0:2])
 
-        w_grp = const.tile([P, n_out, n_t], BF16, align_bytes=64)
-        w_q = const.tile([P, n_out], U32, align_bytes=64)
-        w_s = const.tile([P, n_out], U8, align_bytes=64)
-        nc.vector.tensor_copy(out=w_grp[:, 0:512, :], in_=w_raw[:, :, 0:512].rearrange("p t n -> p n t"))
-        nc.scalar.copy(out=w_grp[:, 512:1024, :], in_=w_raw[:, :, 512:1024].rearrange("p t n -> p n t"))
-        for h in range(2):
+        def weights(h, engine_copy):
+            cols = slice(512 * h, 512 * h + 512)
+            engine_copy(out=w_grp[:, cols, :], in_=w_raw[:, :, cols].rearrange("p t n -> p n t"))
+
+        def weights_q(h):
             cols = slice(512 * h, 512 * h + 512)
             nc.vector.quantize_mx(out=w_q[:, cols].bitcast(FP8X4), scales=w_s[:, cols],
                                   in_=w_grp[:, cols, :].rearrange("p n t -> p (n t)"))
-        bias = const.tile([P, n_out], F32)
-        nc.scalar.copy(out=bias[:], in_=b_bc[:])
-        b_col = const.tile([P, 8], F32)
-        pbt = ps_o.tile([P, P], BF16, tag="po")
-        nc.tensor.transpose(out=pbt[:], in_=b_rows[:], identity=eye[:, 66:194])
-        nc.vector.tensor_copy(out=b_col[:], in_=pbt[:, 0:8])
-
-        fix = const.tile([P, 16, 4, 2, n_t], BF16)
 
         def border_rows():
-            acc_f = ps_a.tile([P, n_t, P], F32, tag="acc")
+            acc_f = ps_a.tile([P, n_t, P], F32, tag="acc_p")
             for t in range(n_t):
                 f = slice(P * t, P * t + P)
                 for q in range(4):
@@ -141,110 +130,103 @@ def tile_graphconvlayer_kernel(tc, X, Wm, b, H, W, out):
                 nc.scalar.copy(out=fix[:, :, q, :, :],
                                in_=acc_f[:, :, 32 * q:32 * q + 32].rearrange("p t (h i) -> p i h t", h=2))
 
-        def quantise(acc, patch, a_q, a_s):
-            grp = work.tile([P, P, n_t], BF16, align_bytes=64, tag="grp")
-            nc.scalar.copy(out=grp[:], in_=acc[:].rearrange("p t n -> p n t"))
-            if patch is not None:
-                dst = grp[:].rearrange("p (b x) t -> p b (x t)", b=2)
-                src = fix[:, patch, :, :, :].rearrange("p (b r) h t -> p b r (h t)", b=2)
-                nc.scalar.copy(out=dst[:, :, 0:8], in_=src[:, :, 0, :])
-                nc.scalar.copy(out=dst[:, :, 248:256], in_=src[:, :, 1, :])
-            nc.vector.quantize_mx(out=a_q.bitcast(FP8X4), scales=a_s, in_=grp[:].rearrange("p n t -> p (n t)"))
-
-        def direct_out(a_q, a_s, dest):
-            o_sb = stage.tile([P, n_out], F32, tag="o_sb")
-            for h in range(2):
-                cols = slice(512 * h, 512 * h + 512)
-                po = ps_o.tile([P, 512], F32, tag="po")
-                nc.tensor.matmul_mx(out=po[:], lhsT=a_q.bitcast(FP8X4), lhsT_scale=a_s,
-                                    rhs=w_q[:, cols].bitcast(FP8X4), rhs_scale=w_s[:, cols],
-                                    start=True, stop=True)
-                nc.vector.tensor_tensor(out=o_sb[:, cols], in0=po[:], in1=bias[:, cols], op=ADD)
-            nc.sync.dma_start(out=dest, in_=o_sb[:])
-
-        copies = [0]
-
-        def transposed_out(a_q4, a_s4, dests):
-            o_tiles = []
-            for u in range(4):
-                o_u = stage.tile([P, n_out], F32, tag="o_sb", name="o_u%d" % u)
-                o_tiles.append(o_u)
-            for h in range(2):
-                o_t = []
-                for q in range(4):
-                    m = 4 * h + q
-                    cols = slice(P * m, P * m + P)
-                    po = ps_o.tile([P, 512], F32, tag="po")
-                    nc.tensor.matmul_mx(out=po[:], lhsT=w_q[:, cols].bitcast(FP8X4), lhsT_scale=w_s[:, cols],
-                                        rhs=a_q4[:].bitcast(FP8X4), rhs_scale=a_s4[:], start=True, stop=True)
-                    o_m = back.tile([P, 512], F32, tag="o_m", name="o_m%d" % q)
-                    nc.scalar.activation(out=o_m[:], in_=po[:], func=mybir.ActivationFunctionType.Identity,
-                                         bias=b_col[:, m:m + 1], scale=1.0)
-                    o_t.append(o_m)
-                for u in range(4):
-                    pt = ps_o.tile([P, 512], F32, tag="po")
-                    for q in range(4):
-                        nc.tensor.transpose(out=pt[:, P * q:P * q + P], in_=o_t[q][:, P * u:P * u + P],
-                                            identity=id32[:])
-                    copies[0] += 1
-                    if copies[0] % V_COPY_EVERY == 0:
-                        nc.vector.tensor_copy(out=o_tiles[u][:, 512 * h:512 * h + 512], in_=pt[:])
-                    else:
-                        nc.scalar.copy(out=o_tiles[u][:, 512 * h:512 * h + 512], in_=pt[:])
-            for u in range(4):
-                nc.sync.dma_start(out=dests[u], in_=o_tiles[u][:])
-
-        def p_block(g):
-            j = g % 8
-            has_up = j > 0
-            has_dn = j < 7
-            acc = ps_a.tile([P, n_t, P], F32, tag="acc")
-            for t in range(n_t):
-                f = slice(P * t, P * t + P)
-                nc.tensor.matmul(acc[:, t, :], lhsT=xs[:, g, f], rhs=adj[:, 32:160],
-                                 start=True, stop=not (has_up or has_dn))
-                if has_up:
-                    nc.tensor.matmul(acc[:, t, 0:32], lhsT=xs[:, g - 1, f], rhs=adj[:, 160:192],
-                                     start=False, stop=not has_dn)
-                if has_dn:
-                    nc.tensor.matmul(acc[:, t, 96:128], lhsT=xs[:, g + 1, f], rhs=adj[:, 0:32],
-                                     start=False, stop=True)
-            return acc
-
-        def z_sums(ci):
+        def row_sums(ci):
             t32 = ts_pool.tile([P, n_feat], F32, tag="t32")
             s32 = ts_pool.tile([P, n_feat], F32, tag="s32")
             nc.vector.tensor_tensor(out=t32[:], in0=xz[:, ci, :], in1=xz[:, ci + 2, :], op=ADD)
             nc.vector.tensor_tensor(out=s32[:], in0=t32[:], in1=xz[:, ci + 1, :], op=ADD)
             return t32, s32
 
-        def z_block(t32, s32):
-            acc = ps_a.tile([P, n_t, P], F32, tag="acc")
+        def neighbour_sums(g, t32, s32):
+            acc_z = ps_a.tile([P, n_t, P], F32, tag="acc_z")
             for t in range(n_t):
                 f = slice(P * t, P * t + P)
-                nc.tensor.matmul(acc[:, t, :], lhsT=t32[:, f], rhs=id32[:],
+                nc.tensor.matmul(acc_z[:, t, :], lhsT=t32[:, f], rhs=id32[:],
                                  is_transpose=True, start=True, stop=False)
-                nc.tensor.matmul(acc[:, t, :], lhsT=s32[:, f], rhs=cyc_up[:],
+                nc.tensor.matmul(acc_z[:, t, :], lhsT=s32[:, f], rhs=cyc_up[:],
                                  is_transpose=True, start=False, stop=False)
-                nc.tensor.matmul(acc[:, t, :], lhsT=s32[:, f], rhs=cyc_dn[:],
+                nc.tensor.matmul(acc_z[:, t, :], lhsT=s32[:, f], rhs=cyc_dn[:],
                                  is_transpose=True, start=False, stop=True)
-            return acc
+            j = g % 8
+            has_up = j > 0
+            has_dn = j < 7
+            acc_p = ps_a.tile([P, n_t, P], F32, tag="acc_p")
+            for t in range(n_t):
+                f = slice(P * t, P * t + P)
+                nc.tensor.matmul(acc_p[:, t, :], lhsT=xs[:, g, f], rhs=adj[:, 32:160],
+                                 start=True, stop=not (has_up or has_dn))
+                if has_up:
+                    nc.tensor.matmul(acc_p[:, t, 0:32], lhsT=xs[:, g - 1, f], rhs=adj[:, 160:192],
+                                     start=False, stop=not has_dn)
+                if has_dn:
+                    nc.tensor.matmul(acc_p[:, t, 96:128], lhsT=xs[:, g + 1, f], rhs=adj[:, 0:32],
+                                     start=False, stop=True)
+            return acc_p, acc_z
 
-        for k in range(4):
-            a_q4 = quad.tile([P, 512], U32, align_bytes=64, tag="a_q4")
-            a_s4 = quad.tile([P, 512], U8, align_bytes=64, tag="a_s4")
-            for u in range(4):
-                i = 4 * k + u
-                sums = z_sums(i)
-                a_q = work.tile([P, P], U32, align_bytes=64, tag="a_q")
-                a_s = work.tile([P, P], U8, align_bytes=64, tag="a_s")
-                quantise(p_block(i), None, a_q[:], a_s[:])
-                direct_out(a_q[:], a_s[:], op_view[:, i, :])
-                if i == 0:
-                    border_rows()
-                cols = slice(P * u, P * u + P)
-                quantise(z_block(sums[0], sums[1]), i, a_q4[:, cols], a_s4[:, cols])
-                if k not in S2_QUADS:
-                    direct_out(a_q4[:, cols], a_s4[:, cols], oz_view[:, i, :])
-            if k in S2_QUADS:
-                transposed_out(a_q4, a_s4, [oz_view[:, 4 * k + u, :] for u in range(4)])
+        def round_out(i, acc_p, acc_z):
+            grp = work.tile([P, 2, P, n_t], BF16, align_bytes=64, tag="grp")
+            nc.scalar.copy(out=grp[:, 1, :, :], in_=acc_z[:].rearrange("p t n -> p n t"))
+            dst = grp[:, 1, :, :].rearrange("p (b x) t -> p b (x t)", b=2)
+            src = fix[:, i, :, :, :].rearrange("p (b r) h t -> p b r (h t)", b=2)
+            nc.scalar.copy(out=dst[:, :, 0:8], in_=src[:, :, 0, :])
+            nc.scalar.copy(out=dst[:, :, 248:256], in_=src[:, :, 1, :])
+            nc.scalar.copy(out=grp[:, 0, :, :], in_=acc_p[:].rearrange("p t n -> p n t"))
+            return grp
+
+        def quantise(grp):
+            a_q = work.tile([P, 2 * P], U32, align_bytes=64, tag="a_q")
+            a_s = work.tile([P, 2 * P], U8, align_bytes=64, tag="a_s")
+            nc.vector.quantize_mx(out=a_q[:].bitcast(FP8X4), scales=a_s[:],
+                                  in_=grp[:].rearrange("p a n t -> p (a n t)"))
+            return a_q, a_s
+
+        def multiply(a_q, a_s):
+            banks = []
+            for a in range(2):
+                nodes = slice(P * a, P * a + P)
+                for h in range(2):
+                    cols = slice(512 * h, 512 * h + 512)
+                    po = ps_o.tile([P, 512], F32, tag="po", name="po%d%d" % (a, h))
+                    nc.tensor.matmul_mx(out=po[:], lhsT=a_q[:, nodes].bitcast(FP8X4), lhsT_scale=a_s[:, nodes],
+                                        rhs=w_q[:, cols].bitcast(FP8X4), rhs_scale=w_s[:, cols],
+                                        start=True, stop=True)
+                    banks.append(po)
+            return banks
+
+        def add_bias_and_store(i, banks):
+            for a in range(2):
+                o_sb = stage.tile([P, n_out], F32, tag="o_sb", name="o_sb%d" % a)
+                for h in range(2):
+                    cols = slice(512 * h, 512 * h + 512)
+                    po = banks[2 * a + h]
+                    if G_HALF is not None and 2 * a + h == G_HALF:
+                        nc.scalar.copy(out=o_sb[:, cols], in_=po[:])
+                        nc.gpsimd.tensor_tensor(out=o_sb[:, cols], in0=o_sb[:, cols], in1=bias[:, cols], op=ADD)
+                    else:
+                        nc.vector.tensor_tensor(out=o_sb[:, cols], in0=po[:], in1=bias[:, cols], op=ADD)
+                dest = op_view[:, i, :] if a == 0 else oz_view[:, i, :]
+                nc.sync.dma_start(out=dest, in_=o_sb[:])
+
+        n_pairs = 16
+        weights(0, nc.vector.tensor_copy)
+        weights(1, nc.scalar.copy)
+        nc.scalar.copy(out=bias[:], in_=b_bc[:])
+        sums = {0: row_sums(0)}
+        weights_q(0)
+        sums[1] = row_sums(1)
+        weights_q(1)
+        border_rows()
+        accs = neighbour_sums(0, sums[0][0], sums[0][1])
+        grp0 = round_out(0, accs[0], accs[1])
+        ready = quantise(grp0)
+        for i in range(n_pairs):
+            if i + 2 < n_pairs:
+                sums[i + 2] = row_sums(i + 2)
+            if i + 1 < n_pairs:
+                accs = neighbour_sums(i + 1, sums[i + 1][0], sums[i + 1][1])
+            banks = multiply(ready[0], ready[1])
+            if i + 1 < n_pairs:
+                grp_next = round_out(i + 1, accs[0], accs[1])
+            add_bias_and_store(i, banks)
+            if i + 1 < n_pairs:
+                ready = quantise(grp_next)

@@ -13,7 +13,7 @@ ADD = mybir.AluOpType.add
 P = 128
 FLOPS = 2 * 4096 * 512 * 1024
 
-G_HALF = None
+G_HALF = 0
 
 
 def tile_graphconvlayer_kernel(tc, X, Wm, b, H, W, out):

@@ -13,7 +13,7 @@ ADD = mybir.AluOpType.add
 P = 128
 FLOPS = 2 * 4096 * 512 * 1024
 
-G_HALF = 0
+G_HALVES = (0,)
 
 
 def tile_graphconvlayer_kernel(tc, X, Wm, b, H, W, out):
@@ -21,27 +21,25 @@ def tile_graphconvlayer_kernel(tc, X, Wm, b, H, W, out):
     n_feat = X.shape[2]
     n_out = Wm.shape[1]
     n_t = n_feat // P
-
-    xp_view = X[0:2].rearrange("b (j p) f -> p (b j) f", p=P)
-    op_view = out[0:2].rearrange("b (j p) n -> p (b j) n", p=P)
-    xz_flat = X[2:4].rearrange("b n f -> (b n) f")
-    xz_view = xz_flat.rearrange("(p i) f -> p i f", i=16)
-    xz_rows = xz_flat.rearrange("(m k) f -> m k f", k=32)
-    oz_view = out[2:4].rearrange("b n f -> (b n) f").rearrange("(p i) n -> p i n", i=16)
     w_view = Wm.rearrange("(t p) n -> p t n", p=P)
+    z_img = 3
+    xz_view = X[z_img].rearrange("(p i) f -> p i f", i=8)
+    xz_rows = X[z_img].rearrange("(r k) f -> r k f", k=32)
+    oz_view = out[z_img].rearrange("(p i) n -> p i n", i=8)
 
     with ExitStack() as ctx:
         const = ctx.enter_context(tc.tile_pool(name="const", bufs=1))
-        ts_pool = ctx.enter_context(tc.tile_pool(name="ts", bufs=3))
+        ts_pool = ctx.enter_context(tc.tile_pool(name="ts", bufs=2))
         work = ctx.enter_context(tc.tile_pool(name="work", bufs=2))
         stage = ctx.enter_context(tc.tile_pool(name="stage", bufs=6))
         ps_a = ctx.enter_context(tc.psum_pool(name="ps_a", bufs=2))
         ps_o = ctx.enter_context(tc.psum_pool(name="ps_o", bufs=4))
         ctx.enter_context(tc.manual_schedule())
 
-        xs = const.tile([P, 16, n_feat], BF16)
-        xz = const.tile([P, 18, n_feat], BF16)
-        xf = const.tile([P, 2, 2, n_feat], BF16)
+        x0 = const.tile([P, 24, n_feat], BF16)
+        x2 = const.tile([P, 21, n_feat], BF16)
+        xz = const.tile([P, 10, n_feat], BF16)
+        xf = const.tile([P, 2, n_feat], BF16)
         w_raw = const.tile([P, n_t, n_out], BF16)
         b_bc = const.tile([P, n_out], BF16)
         eye = const.tile([P, 260], BF16)
@@ -59,26 +57,41 @@ def tile_graphconvlayer_kernel(tc, X, Wm, b, H, W, out):
         w_q = const.tile([P, n_out], U32, align_bytes=64)
         w_s = const.tile([P, n_out], U8, align_bytes=64)
         bias = const.tile([P, n_out], F32)
-        fix = const.tile([P, 16, 4, 2, n_t], BF16)
+        fix = const.tile([P, 8, 2, 4, n_t], BF16)
+
+        def load_x0(img, lo, hi):
+            nc.sync.dma_start(out=x0[:, 8 * img + lo:8 * img + hi, :],
+                              in_=X[img, P * lo:P * hi, :].rearrange("(j p) f -> p j f", p=P))
+
+        def load_x2(img, lo, hi):
+            nc.sync.dma_start(out=x2[:, 7 * img + lo:7 * img + hi, :],
+                              in_=X[img, 64 + P * lo:64 + P * hi, :].rearrange("(j p) f -> p j f", p=P))
 
         nc.vector.memset(xz[:, 0, :], 0.0)
-        nc.vector.memset(xz[:, 17, :], 0.0)
-        nc.scalar.dma_start(out=b_bc[:], in_=b.partition_broadcast(P))
+        nc.vector.memset(xz[:, 9, :], 0.0)
+        load_x0(0, 0, 2)
+        load_x2(0, 0, 2)
         nc.sync.dma_start(out=w_raw[:, :, 0:512], in_=w_view[:, :, 0:512])
-        nc.sync.dma_start(out=xs[:, 0:2, :], in_=xp_view[:, 0:2, :])
-        nc.sync.dma_start(out=xz[1:128:2, 0, :], in_=xz_rows[:, 15, :])
-        nc.sync.dma_start(out=xz[:, 1:5, :], in_=xz_view[:, 0:4, :])
         nc.sync.dma_start(out=w_raw[:, :, 512:1024], in_=w_view[:, :, 512:1024])
-        nc.sync.dma_start(out=xf[:, 0, :, :], in_=X[2:4, 0:128, :].rearrange("b p f -> p b f"))
-        nc.sync.dma_start(out=xf[:, 1, :, :], in_=X[2:4, 896:1024, :].rearrange("b p f -> p b f"))
-        nc.sync.dma_start(out=xs[:, 2:4, :], in_=xp_view[:, 2:4, :])
-        nc.sync.dma_start(out=xs[:, 4:8, :], in_=xp_view[:, 4:8, :])
+        nc.scalar.dma_start(out=b_bc[:], in_=b.partition_broadcast(P))
+        load_x0(0, 2, 4)
+        load_x2(0, 2, 4)
+        nc.sync.dma_start(out=xz[:, 1:5, :], in_=xz_view[:, 0:4, :])
+        for cq in range(1, 4):
+            nc.sync.dma_start(out=xz[cq:128:4, 0, :], in_=xz_rows[:, 8 * cq - 1, :])
+        nc.sync.dma_start(out=xf[:, 0, :], in_=X[z_img, 0:128, :])
+        nc.sync.dma_start(out=xf[:, 1, :], in_=X[z_img, 896:1024, :])
+        load_x0(0, 4, 8)
+        load_x2(0, 4, 7)
         nc.sync.dma_start(out=xz[:, 5:9, :], in_=xz_view[:, 4:8, :])
-        nc.sync.dma_start(out=xs[:, 8:12, :], in_=xp_view[:, 8:12, :])
-        nc.sync.dma_start(out=xz[:, 9:13, :], in_=xz_view[:, 8:12, :])
-        nc.sync.dma_start(out=xs[:, 12:16, :], in_=xp_view[:, 12:16, :])
-        nc.sync.dma_start(out=xz[:, 13:17, :], in_=xz_view[:, 12:16, :])
-        nc.sync.dma_start(out=xz[0:128:2, 17, :], in_=xz_rows[:, 16, :])
+        for cq in range(0, 3):
+            nc.sync.dma_start(out=xz[cq:128:4, 9, :], in_=xz_rows[:, 8 * cq + 8, :])
+
+        later_loads = {0: (1, 0), 2: (1, 1), 4: (2, 0), 6: (2, 1)}
+
+        def load_half_image(img, half):
+            load_x0(img, 4 * half, 4 * half + 4)
+            load_x2(img, 4 * half, min(4 * half + 4, 7))
 
         nc.vector.memset(idx[:, 0:1], 0.0)
         for w in (1, 2, 4, 8, 16, 32, 64, 128, 256):
@@ -102,33 +115,34 @@ def tile_graphconvlayer_kernel(tc, X, Wm, b, H, W, out):
             out=adj[:].rearrange("p (r c) -> p r c", c=32)[:, :, 31:32],
             in_=a1[:].rearrange("p (r c) -> p r c", c=32)[:, :, 31:32],
         )
-        nc.vector.tensor_copy(out=id32[:], in_=eye[:, 66:194])
-        nc.vector.tensor_copy(out=cyc_up[:, 2:128], in_=id32[:, 0:126])
-        nc.vector.tensor_copy(out=cyc_up[:, 0:2], in_=id32[:, 126:128])
-        nc.vector.tensor_copy(out=cyc_dn[:, 0:126], in_=id32[:, 2:128])
-        nc.vector.tensor_copy(out=cyc_dn[:, 126:128], in_=id32[:, 0:2])
 
-        def weights(h, engine_copy):
-            cols = slice(512 * h, 512 * h + 512)
-            engine_copy(out=w_grp[:, cols, :], in_=w_raw[:, :, cols].rearrange("p t n -> p n t"))
+        def regroup(copy, lo, hi):
+            copy(out=w_grp[:, lo:hi, :], in_=w_raw[:, :, lo:hi].rearrange("p t n -> p n t"))
 
         def weights_q(h):
             cols = slice(512 * h, 512 * h + 512)
             nc.vector.quantize_mx(out=w_q[:, cols].bitcast(FP8X4), scales=w_s[:, cols],
                                   in_=w_grp[:, cols, :].rearrange("p n t -> p (n t)"))
 
-        def border_rows():
-            acc_f = ps_a.tile([P, n_t, P], F32, tag="acc_p")
+        def shifts():
+            nc.vector.tensor_copy(out=id32[:], in_=eye[:, 66:194])
+            nc.vector.tensor_copy(out=cyc_up[:, 4:128], in_=id32[:, 0:124])
+            nc.vector.tensor_copy(out=cyc_up[:, 0:4], in_=id32[:, 124:128])
+            nc.vector.tensor_copy(out=cyc_dn[:, 0:124], in_=id32[:, 4:128])
+            nc.vector.tensor_copy(out=cyc_dn[:, 124:128], in_=id32[:, 0:4])
+
+        def border_rows_sum():
+            acc_f = ps_a.tile([P, n_t, P], F32, tag="acc1")
             for t in range(n_t):
                 f = slice(P * t, P * t + P)
-                for q in range(4):
-                    rr = q % 2
-                    a_cols = slice(32, 64) if rr == 0 else slice(128, 160)
-                    nc.tensor.matmul(acc_f[:, t, 32 * q:32 * q + 32], lhsT=xf[:, rr, q // 2, f], rhs=adj[:, a_cols],
-                                     start=True, stop=True)
-            for q in range(4):
-                nc.scalar.copy(out=fix[:, :, q, :, :],
-                               in_=acc_f[:, :, 32 * q:32 * q + 32].rearrange("p t (h i) -> p i h t", h=2))
+                nc.tensor.matmul(acc_f[:, t, 0:32], lhsT=xf[:, 0, f], rhs=adj[:, 32:64], start=True, stop=True)
+                nc.tensor.matmul(acc_f[:, t, 32:64], lhsT=xf[:, 1, f], rhs=adj[:, 128:160], start=True, stop=True)
+            return acc_f
+
+        def border_rows_round(acc_f):
+            for rr in range(2):
+                nc.scalar.copy(out=fix[:, :, rr, :, :],
+                               in_=acc_f[:, :, 32 * rr:32 * rr + 32].rearrange("p t (q i) -> p i q t", q=4))
 
         def row_sums(ci):
             t32 = ts_pool.tile([P, n_feat], F32, tag="t32")
@@ -137,40 +151,58 @@ def tile_graphconvlayer_kernel(tc, X, Wm, b, H, W, out):
             nc.vector.tensor_tensor(out=s32[:], in0=t32[:], in1=xz[:, ci + 1, :], op=ADD)
             return t32, s32
 
-        def neighbour_sums(g, t32, s32):
-            acc_z = ps_a.tile([P, n_t, P], F32, tag="acc_z")
+        def z_sum(acc, t32, s32):
             for t in range(n_t):
                 f = slice(P * t, P * t + P)
-                nc.tensor.matmul(acc_z[:, t, :], lhsT=t32[:, f], rhs=id32[:],
-                                 is_transpose=True, start=True, stop=False)
-                nc.tensor.matmul(acc_z[:, t, :], lhsT=s32[:, f], rhs=cyc_up[:],
-                                 is_transpose=True, start=False, stop=False)
-                nc.tensor.matmul(acc_z[:, t, :], lhsT=s32[:, f], rhs=cyc_dn[:],
-                                 is_transpose=True, start=False, stop=True)
-            j = g % 8
-            has_up = j > 0
-            has_dn = j < 7
-            acc_p = ps_a.tile([P, n_t, P], F32, tag="acc_p")
-            for t in range(n_t):
-                f = slice(P * t, P * t + P)
-                nc.tensor.matmul(acc_p[:, t, :], lhsT=xs[:, g, f], rhs=adj[:, 32:160],
-                                 start=True, stop=not (has_up or has_dn))
-                if has_up:
-                    nc.tensor.matmul(acc_p[:, t, 0:32], lhsT=xs[:, g - 1, f], rhs=adj[:, 160:192],
-                                     start=False, stop=not has_dn)
-                if has_dn:
-                    nc.tensor.matmul(acc_p[:, t, 96:128], lhsT=xs[:, g + 1, f], rhs=adj[:, 0:32],
-                                     start=False, stop=True)
-            return acc_p, acc_z
+                nc.tensor.matmul(acc[:, t, :], lhsT=t32[:, f], rhs=id32[:], is_transpose=True, start=True, stop=False)
+                nc.tensor.matmul(acc[:, t, :], lhsT=s32[:, f], rhs=cyc_up[:], is_transpose=True, start=False, stop=False)
+                nc.tensor.matmul(acc[:, t, :], lhsT=s32[:, f], rhs=cyc_dn[:], is_transpose=True, start=False, stop=True)
 
-        def round_out(i, acc_p, acc_z):
+        def p_parts(n):
+            img = n // 8
+            u = n % 8
+            if u < 7:
+                return [(x0, 8 * img + u, 64, 0, 64), (x2, 7 * img + u, 64, 64, 64)]
+            return [(x0, 8 * img, 32, 0, 32), (x0, 8 * img + 7, 64, 32, 64), (x0, 8 * img + 7, 128, 96, 32)]
+
+        def p_sum(acc, n):
+            for t in range(n_t):
+                f = slice(P * t, P * t + P)
+                for (src, blk, a_lo, o_lo, width) in p_parts(n):
+                    nc.tensor.matmul(acc[:, t, o_lo:o_lo + width], lhsT=src[:, blk, f], rhs=adj[:, a_lo:a_lo + width],
+                                     start=True, stop=True)
+
+        def p_stores(n):
+            img = n // 8
+            u = n % 8
+            if u < 7:
+                return [(0, P, out[img, P * u + 32:P * u + 160, :])]
+            return [(0, 32, out[img, 0:32, :]), (32, 96, out[img, 928:992, :]), (96, P, out[img, 992:1024, :])]
+
+        def pair_tiles(s):
+            m = s // 2
+            if s % 2 == 0:
+                return [("p", 3 * m), ("p", 3 * m + 1)]
+            return [("p", 3 * m + 2), ("z", m)]
+
+        def neighbour_sums(s, sums):
+            accs = []
+            for a, (kind, n) in enumerate(pair_tiles(s)):
+                acc = ps_a.tile([P, n_t, P], F32, tag="acc%d" % a, name="acc%d" % a)
+                if kind == "p":
+                    p_sum(acc, n)
+                else:
+                    z_sum(acc, sums[n][0], sums[n][1])
+                accs.append(acc)
+            return accs
+
+        def round_out(s, accs):
             grp = work.tile([P, 2, P, n_t], BF16, align_bytes=64, tag="grp")
-            nc.scalar.copy(out=grp[:, 1, :, :], in_=acc_z[:].rearrange("p t n -> p n t"))
-            dst = grp[:, 1, :, :].rearrange("p (b x) t -> p b (x t)", b=2)
-            src = fix[:, i, :, :, :].rearrange("p (b r) h t -> p b r (h t)", b=2)
-            nc.scalar.copy(out=dst[:, :, 0:8], in_=src[:, :, 0, :])
-            nc.scalar.copy(out=dst[:, :, 248:256], in_=src[:, :, 1, :])
-            nc.scalar.copy(out=grp[:, 0, :, :], in_=acc_p[:].rearrange("p t n -> p n t"))
+            for a, (kind, n) in enumerate(pair_tiles(s)):
+                nc.scalar.copy(out=grp[:, a, :, :], in_=accs[a][:].rearrange("p t n -> p n t"))
+                if kind == "z":
+                    nc.scalar.copy(out=grp[:, a, 0:4, :], in_=fix[:, n, 0, :, :])
+                    nc.scalar.copy(out=grp[:, a, 124:128, :], in_=fix[:, n, 1, :, :])
             return grp
 
         def quantise(grp):
@@ -182,51 +214,65 @@ def tile_graphconvlayer_kernel(tc, X, Wm, b, H, W, out):
 
         def multiply(a_q, a_s):
             banks = []
-            for a in range(2):
-                nodes = slice(P * a, P * a + P)
-                for h in range(2):
-                    cols = slice(512 * h, 512 * h + 512)
-                    po = ps_o.tile([P, 512], F32, tag="po", name="po%d%d" % (a, h))
+            for h in range(2):
+                cols = slice(512 * h, 512 * h + 512)
+                for a in range(2):
+                    nodes = slice(P * a, P * a + P)
+                    po = ps_o.tile([P, 512], F32, tag="po", name="po%d%d" % (h, a))
                     nc.tensor.matmul_mx(out=po[:], lhsT=a_q[:, nodes].bitcast(FP8X4), lhsT_scale=a_s[:, nodes],
                                         rhs=w_q[:, cols].bitcast(FP8X4), rhs_scale=w_s[:, cols],
                                         start=True, stop=True)
                     banks.append(po)
             return banks
 
-        def add_bias_and_store(i, banks):
+        def add_bias_and_store(s, banks):
+            o_tiles = []
             for a in range(2):
-                o_sb = stage.tile([P, n_out], F32, tag="o_sb", name="o_sb%d" % a)
-                for h in range(2):
-                    cols = slice(512 * h, 512 * h + 512)
-                    po = banks[2 * a + h]
-                    if G_HALF is not None and 2 * a + h == G_HALF:
+                o_new = stage.tile([P, n_out], F32, tag="o_sb", name="o_sb%d" % a)
+                o_tiles.append(o_new)
+            for h in range(2):
+                cols = slice(512 * h, 512 * h + 512)
+                for a in range(2):
+                    po = banks[2 * h + a]
+                    o_sb = o_tiles[a]
+                    if 2 * h + a in G_HALVES:
                         nc.scalar.copy(out=o_sb[:, cols], in_=po[:])
                         nc.gpsimd.tensor_tensor(out=o_sb[:, cols], in0=o_sb[:, cols], in1=bias[:, cols], op=ADD)
                     else:
                         nc.vector.tensor_tensor(out=o_sb[:, cols], in0=po[:], in1=bias[:, cols], op=ADD)
-                dest = op_view[:, i, :] if a == 0 else oz_view[:, i, :]
-                nc.sync.dma_start(out=dest, in_=o_sb[:])
+            for a, (kind, n) in enumerate(pair_tiles(s)):
+                o_sb = o_tiles[a]
+                if kind == "z":
+                    nc.sync.dma_start(out=oz_view[:, n, :], in_=o_sb[:])
+                else:
+                    for (lo, hi, dest) in p_stores(n):
+                        nc.sync.dma_start(out=dest, in_=o_sb[lo:hi, :])
 
         n_pairs = 16
-        weights(0, nc.vector.tensor_copy)
-        weights(1, nc.scalar.copy)
-        nc.scalar.copy(out=bias[:], in_=b_bc[:])
-        sums = {0: row_sums(0)}
+        sums = {}
+        regroup(nc.vector.tensor_copy, 0, 512)
         weights_q(0)
-        sums[1] = row_sums(1)
+        accs = neighbour_sums(0, sums)
+        grp_next = round_out(0, accs)
+        regroup(nc.scalar.copy, 768, 1024)
+        nc.scalar.copy(out=bias[:], in_=b_bc[:])
+        regroup(nc.vector.tensor_copy, 512, 768)
+        shifts()
+        ready = quantise(grp_next)
         weights_q(1)
-        border_rows()
-        accs = neighbour_sums(0, sums[0][0], sums[0][1])
-        grp0 = round_out(0, accs[0], accs[1])
-        ready = quantise(grp0)
-        for i in range(n_pairs):
-            if i + 2 < n_pairs:
-                sums[i + 2] = row_sums(i + 2)
-            if i + 1 < n_pairs:
-                accs = neighbour_sums(i + 1, sums[i + 1][0], sums[i + 1][1])
+        sums[0] = row_sums(0)
+        acc_f = border_rows_sum()
+        border_rows_round(acc_f)
+        for s in range(n_pairs):
+            if (s + 2) % 2 == 1 and s + 2 < n_pairs:
+                sums[(s + 2) // 2] = row_sums((s + 2) // 2)
+            if s + 1 < n_pairs:
+                accs = neighbour_sums(s + 1, sums)
             banks = multiply(ready[0], ready[1])
-            if i + 1 < n_pairs:
-                grp_next = round_out(i + 1, accs[0], accs[1])
-            add_bias_and_store(i, banks)
-            if i + 1 < n_pairs:
+            if s + 1 < n_pairs:
+                grp_next = round_out(s + 1, accs)
+            add_bias_and_store(s, banks)
+            if s in later_loads:
+                load_half_image(later_loads[s][0], later_loads[s][1])
+            if s + 1 < n_pairs:
                 ready = quantise(grp_next)

@@ -13,6 +13,7 @@ ADD = mybir.AluOpType.add
 P = 128
 FLOPS = 2 * 4096 * 512 * 1024
 
+PAIR_KINDS = "AAABABABABABABBB"
 G_HALVES = (0,)
 
 
@@ -29,9 +30,9 @@ def tile_graphconvlayer_kernel(tc, X, Wm, b, H, W, out):
 
     with ExitStack() as ctx:
         const = ctx.enter_context(tc.tile_pool(name="const", bufs=1))
-        ts_pool = ctx.enter_context(tc.tile_pool(name="ts", bufs=2))
+        ts_pool = ctx.enter_context(tc.tile_pool(name="ts", bufs=3))
         work = ctx.enter_context(tc.tile_pool(name="work", bufs=2))
-        stage = ctx.enter_context(tc.tile_pool(name="stage", bufs=6))
+        stage = ctx.enter_context(tc.tile_pool(name="stage", bufs=8))
         ps_a = ctx.enter_context(tc.psum_pool(name="ps_a", bufs=2))
         ps_o = ctx.enter_context(tc.psum_pool(name="ps_o", bufs=4))
         ctx.enter_context(tc.manual_schedule())
@@ -42,14 +43,13 @@ def tile_graphconvlayer_kernel(tc, X, Wm, b, H, W, out):
         xf = const.tile([P, 2, n_feat], BF16)
         w_raw = const.tile([P, n_t, n_out], BF16)
         b_bc = const.tile([P, n_out], BF16)
-        eye = const.tile([P, 260], BF16)
         id32 = const.tile([P, P], F32)
-        idx = const.tile([P, 260], F32, align_bytes=64)
+        idx = const.tile([P, 32], F32, align_bytes=64)
         low = const.tile([P, 32], F32, align_bytes=64)
-        pos = const.tile([P, 1], F32)
-        r2 = const.tile([P, 194], BF16)
-        r3 = const.tile([P, 194], BF16)
-        a1 = const.tile([P, 192], BF16)
+        dif = const.tile([P, 32], F32)
+        sq = const.tile([P, 32], F32)
+        pat = const.tile([P, 96], BF16)
+        blk = const.tile([P, 32], F32)
         adj = const.tile([P, 192], BF16)
         cyc_up = const.tile([P, P], F32)
         cyc_dn = const.tile([P, P], F32)
@@ -76,45 +76,40 @@ def tile_graphconvlayer_kernel(tc, X, Wm, b, H, W, out):
         nc.scalar.dma_start(out=b_bc[:], in_=b.partition_broadcast(P))
         load_x0(0, 2, 4)
         load_x2(0, 2, 4)
+        load_x0(0, 4, 8)
+        load_x2(0, 4, 7)
         nc.sync.dma_start(out=xz[:, 1:5, :], in_=xz_view[:, 0:4, :])
         for cq in range(1, 4):
             nc.sync.dma_start(out=xz[cq:128:4, 0, :], in_=xz_rows[:, 8 * cq - 1, :])
         nc.sync.dma_start(out=xf[:, 0, :], in_=X[z_img, 0:128, :])
         nc.sync.dma_start(out=xf[:, 1, :], in_=X[z_img, 896:1024, :])
-        load_x0(0, 4, 8)
-        load_x2(0, 4, 7)
+        load_x0(1, 0, 4)
+        load_x2(1, 0, 4)
         nc.sync.dma_start(out=xz[:, 5:9, :], in_=xz_view[:, 4:8, :])
         for cq in range(0, 3):
             nc.sync.dma_start(out=xz[cq:128:4, 9, :], in_=xz_rows[:, 8 * cq + 8, :])
 
-        later_loads = {0: (1, 0), 2: (1, 1), 4: (2, 0), 6: (2, 1)}
+        later_loads = {0: (1, 1), 2: (2, 0), 5: (2, 1)}
 
         def load_half_image(img, half):
             load_x0(img, 4 * half, 4 * half + 4)
             load_x2(img, 4 * half, min(4 * half + 4, 7))
 
+        nc.vector.memset(adj[:], 0.0)
+        nc.vector.memset(id32[:], 0.0)
         nc.vector.memset(idx[:, 0:1], 0.0)
-        for w in (1, 2, 4, 8, 16, 32, 64, 128, 256):
-            n = min(w, 260 - w)
-            nc.vector.tensor_scalar_add(out=idx[:, w:w + n], in0=idx[:, 0:n], scalar1=float(w))
-        nc.vector.transpose(out=low[:], in_=idx[:, 0:32])
-        for q in range(4):
-            rows = slice(32 * q, 32 * q + 32)
-            nc.vector.tensor_scalar_add(out=pos[rows, :], in0=low[rows, 0:1], scalar1=float(32 * q + 66))
-        nc.vector.tensor_scalar(out=eye[:], in0=idx[:], scalar1=pos[:, 0:1], scalar2=None,
-                                op0=mybir.AluOpType.is_equal)
-        nc.vector.tensor_tensor(out=r2[:], in0=eye[:, 1:195], in1=eye[:, 65:259], op=ADD)
-        nc.vector.tensor_tensor(out=r3[:], in0=r2[:], in1=eye[:, 33:227], op=ADD)
-        nc.vector.tensor_tensor(out=a1[:], in0=r2[:, 1:193], in1=r3[:, 0:192], op=ADD)
-        nc.vector.tensor_copy(
-            out=a1[:].rearrange("p (r c) -> p r c", c=32)[:, :, 0:1],
-            in_=r2[:, 1:193].rearrange("p (r c) -> p r c", c=32)[:, :, 0:1],
-        )
-        nc.vector.tensor_tensor(out=adj[:], in0=a1[:], in1=r3[:, 2:194], op=ADD)
-        nc.vector.tensor_copy(
-            out=adj[:].rearrange("p (r c) -> p r c", c=32)[:, :, 31:32],
-            in_=a1[:].rearrange("p (r c) -> p r c", c=32)[:, :, 31:32],
-        )
+        for w in (1, 2, 4, 8, 16):
+            nc.vector.tensor_scalar_add(out=idx[:, w:2 * w], in0=idx[:, 0:w], scalar1=float(w))
+        nc.vector.transpose(out=low[:], in_=idx[:])
+        nc.vector.tensor_scalar(out=dif[:], in0=idx[:], scalar1=low[:, 0:1], scalar2=None,
+                                op0=mybir.AluOpType.subtract)
+        nc.vector.tensor_tensor(out=sq[:], in0=dif[:], in1=dif[:], op=mybir.AluOpType.mult)
+        nc.vector.tensor_scalar(out=pat[:, 0:32], in0=sq[:], scalar1=1.0, scalar2=None, op0=mybir.AluOpType.is_le)
+        nc.vector.tensor_scalar(out=pat[:, 32:64], in0=sq[:], scalar1=1.0, scalar2=None, op0=mybir.AluOpType.is_equal)
+        nc.vector.tensor_scalar(out=pat[:, 64:96], in0=sq[:], scalar1=1.0, scalar2=None, op0=mybir.AluOpType.is_le)
+        for rl in range(4):
+            rows = slice(32 * rl, 32 * rl + 32)
+            nc.vector.tensor_copy(out=adj[rows, 32 * rl:32 * rl + 96], in_=pat[rows, :])
 
         def regroup(copy, lo, hi):
             copy(out=w_grp[:, lo:hi, :], in_=w_raw[:, :, lo:hi].rearrange("p t n -> p n t"))
@@ -125,7 +120,10 @@ def tile_graphconvlayer_kernel(tc, X, Wm, b, H, W, out):
                                   in_=w_grp[:, cols, :].rearrange("p n t -> p (n t)"))
 
         def shifts():
-            nc.vector.tensor_copy(out=id32[:], in_=eye[:, 66:194])
+            nc.vector.tensor_scalar(out=blk[:], in0=sq[:], scalar1=0.0, scalar2=None, op0=mybir.AluOpType.is_equal)
+            for q in range(4):
+                rows = slice(32 * q, 32 * q + 32)
+                nc.vector.tensor_copy(out=id32[rows, 32 * q:32 * q + 32], in_=blk[rows, :])
             nc.vector.tensor_copy(out=cyc_up[:, 4:128], in_=id32[:, 0:124])
             nc.vector.tensor_copy(out=cyc_up[:, 0:4], in_=id32[:, 124:128])
             nc.vector.tensor_copy(out=cyc_dn[:, 0:124], in_=id32[:, 4:128])
@@ -179,11 +177,22 @@ def tile_graphconvlayer_kernel(tc, X, Wm, b, H, W, out):
                 return [(0, P, out[img, P * u + 32:P * u + 160, :])]
             return [(0, 32, out[img, 0:32, :]), (32, 96, out[img, 928:992, :]), (96, P, out[img, 992:1024, :])]
 
+        pairs = []
+        first_use = {}
+        n_p = 0
+        n_z = 0
+        for s, kind in enumerate(PAIR_KINDS):
+            if kind == "A":
+                pairs.append([("p", n_p), ("p", n_p + 1)])
+                n_p += 2
+            else:
+                pairs.append([("p", n_p), ("z", n_z)])
+                first_use[s] = n_z
+                n_p += 1
+                n_z += 1
+
         def pair_tiles(s):
-            m = s // 2
-            if s % 2 == 0:
-                return [("p", 3 * m), ("p", 3 * m + 1)]
-            return [("p", 3 * m + 2), ("z", m)]
+            return pairs[s]
 
         def neighbour_sums(s, sums):
             accs = []
@@ -196,14 +205,12 @@ def tile_graphconvlayer_kernel(tc, X, Wm, b, H, W, out):
                 accs.append(acc)
             return accs
 
-        def round_out(s, accs):
-            grp = work.tile([P, 2, P, n_t], BF16, align_bytes=64, tag="grp")
-            for a, (kind, n) in enumerate(pair_tiles(s)):
-                nc.scalar.copy(out=grp[:, a, :, :], in_=accs[a][:].rearrange("p t n -> p n t"))
-                if kind == "z":
-                    nc.scalar.copy(out=grp[:, a, 0:4, :], in_=fix[:, n, 0, :, :])
-                    nc.scalar.copy(out=grp[:, a, 124:128, :], in_=fix[:, n, 1, :, :])
-            return grp
+        def round_out(s, a, accs, grp):
+            kind, n = pair_tiles(s)[a]
+            nc.scalar.copy(out=grp[:, a, :, :], in_=accs[a][:].rearrange("p t n -> p n t"))
+            if kind == "z":
+                nc.scalar.copy(out=grp[:, a, 0:4, :], in_=fix[:, n, 0, :, :])
+                nc.scalar.copy(out=grp[:, a, 124:128, :], in_=fix[:, n, 1, :, :])
 
         def quantise(grp):
             a_q = work.tile([P, 2 * P], U32, align_bytes=64, tag="a_q")
@@ -225,54 +232,68 @@ def tile_graphconvlayer_kernel(tc, X, Wm, b, H, W, out):
                     banks.append(po)
             return banks
 
-        def add_bias_and_store(s, banks):
+        def out_tiles():
             o_tiles = []
             for a in range(2):
                 o_new = stage.tile([P, n_out], F32, tag="o_sb", name="o_sb%d" % a)
                 o_tiles.append(o_new)
-            for h in range(2):
-                cols = slice(512 * h, 512 * h + 512)
-                for a in range(2):
-                    po = banks[2 * h + a]
-                    o_sb = o_tiles[a]
-                    if 2 * h + a in G_HALVES:
-                        nc.scalar.copy(out=o_sb[:, cols], in_=po[:])
-                        nc.gpsimd.tensor_tensor(out=o_sb[:, cols], in0=o_sb[:, cols], in1=bias[:, cols], op=ADD)
-                    else:
-                        nc.vector.tensor_tensor(out=o_sb[:, cols], in0=po[:], in1=bias[:, cols], op=ADD)
-            for a, (kind, n) in enumerate(pair_tiles(s)):
-                o_sb = o_tiles[a]
-                if kind == "z":
-                    nc.sync.dma_start(out=oz_view[:, n, :], in_=o_sb[:])
-                else:
-                    for (lo, hi, dest) in p_stores(n):
-                        nc.sync.dma_start(out=dest, in_=o_sb[lo:hi, :])
+            return o_tiles
 
-        n_pairs = 16
+        def add_bias(k, banks, o_tiles):
+            cols = slice(512 * (k // 2), 512 * (k // 2) + 512)
+            o_sb = o_tiles[k % 2]
+            if k in G_HALVES:
+                nc.scalar.copy(out=o_sb[:, cols], in_=banks[k][:])
+                nc.gpsimd.tensor_tensor(out=o_sb[:, cols], in0=o_sb[:, cols], in1=bias[:, cols], op=ADD)
+            else:
+                nc.vector.tensor_tensor(out=o_sb[:, cols], in0=banks[k][:], in1=bias[:, cols], op=ADD)
+
+        def store(s, a, o_tiles):
+            kind, n = pair_tiles(s)[a]
+            if kind == "z":
+                nc.sync.dma_start(out=oz_view[:, n, :], in_=o_tiles[a][:])
+            else:
+                for (lo, hi, dest) in p_stores(n):
+                    nc.sync.dma_start(out=dest, in_=o_tiles[a][lo:hi, :])
+
+        n_pairs = len(PAIR_KINDS)
         sums = {}
+        shifts()
         regroup(nc.vector.tensor_copy, 0, 512)
         weights_q(0)
         accs = neighbour_sums(0, sums)
-        grp_next = round_out(0, accs)
+        grp_next = work.tile([P, 2, P, n_t], BF16, align_bytes=64, tag="grp")
+        round_out(0, 0, accs, grp_next)
+        round_out(0, 1, accs, grp_next)
         regroup(nc.scalar.copy, 768, 1024)
         nc.scalar.copy(out=bias[:], in_=b_bc[:])
         regroup(nc.vector.tensor_copy, 512, 768)
-        shifts()
         ready = quantise(grp_next)
         weights_q(1)
-        sums[0] = row_sums(0)
-        acc_f = border_rows_sum()
-        border_rows_round(acc_f)
         for s in range(n_pairs):
-            if (s + 2) % 2 == 1 and s + 2 < n_pairs:
-                sums[(s + 2) // 2] = row_sums((s + 2) // 2)
-            if s + 1 < n_pairs:
+            more = s + 1 < n_pairs
+            if more:
                 accs = neighbour_sums(s + 1, sums)
             banks = multiply(ready[0], ready[1])
-            if s + 1 < n_pairs:
-                grp_next = round_out(s + 1, accs)
-            add_bias_and_store(s, banks)
+            if s == 1:
+                acc_f = border_rows_sum()
+            o_tiles = out_tiles()
+            if more:
+                grp_next = work.tile([P, 2, P, n_t], BF16, align_bytes=64, tag="grp")
+                round_out(s + 1, 0, accs, grp_next)
+            add_bias(0, banks, o_tiles)
+            if more:
+                round_out(s + 1, 1, accs, grp_next)
+            if s == 1:
+                border_rows_round(acc_f)
+            add_bias(1, banks, o_tiles)
+            add_bias(2, banks, o_tiles)
+            store(s, 0, o_tiles)
+            if more:
+                ready = quantise(grp_next)
+            add_bias(3, banks, o_tiles)
+            store(s, 1, o_tiles)
             if s in later_loads:
                 load_half_image(later_loads[s][0], later_loads[s][1])
-            if s + 1 < n_pairs:
-                ready = quantise(grp_next)
+            if s + 3 in first_use:
+                sums[first_use[s + 3]] = row_sums(first_use[s + 3])

@@ -30,7 +30,7 @@ def tile_graphconvlayer_kernel(tc, X, Wm, b, H, W, out):
 
     with ExitStack() as ctx:
         const = ctx.enter_context(tc.tile_pool(name="const", bufs=1))
-        ts_pool = ctx.enter_context(tc.tile_pool(name="ts", bufs=3))
+        ts_pool = ctx.enter_context(tc.tile_pool(name="ts", bufs=4))
         work = ctx.enter_context(tc.tile_pool(name="work", bufs=2))
         stage = ctx.enter_context(tc.tile_pool(name="stage", bufs=8))
         ps_a = ctx.enter_context(tc.psum_pool(name="ps_a", bufs=2))
@@ -270,6 +270,9 @@ def tile_graphconvlayer_kernel(tc, X, Wm, b, H, W, out):
         regroup(nc.vector.tensor_copy, 512, 768)
         ready = quantise(grp_next)
         weights_q(1)
+        sums_after = {}
+        for s in sorted(first_use):
+            sums_after[max(s - 4, 0)] = first_use[s]
         for s in range(n_pairs):
             more = s + 1 < n_pairs
             if more:
@@ -281,19 +284,17 @@ def tile_graphconvlayer_kernel(tc, X, Wm, b, H, W, out):
             if more:
                 grp_next = work.tile([P, 2, P, n_t], BF16, align_bytes=64, tag="grp")
                 round_out(s + 1, 0, accs, grp_next)
-            add_bias(0, banks, o_tiles)
-            if more:
                 round_out(s + 1, 1, accs, grp_next)
+                ready = quantise(grp_next)
+            add_bias(0, banks, o_tiles)
             if s == 1:
                 border_rows_round(acc_f)
             add_bias(1, banks, o_tiles)
             add_bias(2, banks, o_tiles)
             store(s, 0, o_tiles)
-            if more:
-                ready = quantise(grp_next)
             add_bias(3, banks, o_tiles)
             store(s, 1, o_tiles)
             if s in later_loads:
                 load_half_image(later_loads[s][0], later_loads[s][1])
-            if s + 3 in first_use:
-                sums[first_use[s + 3]] = row_sums(first_use[s + 3])
+            if s in sums_after:
+                sums[sums_after[s]] = row_sums(sums_after[s])

from contextlib import ExitStack

import concourse.mybir as mybir
from concourse.masks import make_identity

BF16 = mybir.dt.bfloat16
F32 = mybir.dt.float32
U32 = mybir.dt.uint32
U8 = mybir.dt.uint8
FP8X4 = mybir.dt.float8_e4m3fn_x4
ADD = mybir.AluOpType.add

P = 128
FLOPS = 2 * 4096 * 512 * 1024

PAIR_KINDS = "AAABABABABABABBB"
G_HALVES = (0,)


def tile_graphconvlayer_kernel(tc, X, Wm, b, H, W, out):
    nc = tc.nc
    n_feat = X.shape[2]
    n_out = Wm.shape[1]
    n_t = n_feat // P
    w_view = Wm.rearrange("(t p) n -> p t n", p=P)
    z_img = 3
    xz_view = X[z_img].rearrange("(p i) f -> p i f", i=8)
    xz_rows = X[z_img].rearrange("(r k) f -> r k f", k=32)
    oz_view = out[z_img].rearrange("(p i) n -> p i n", i=8)

    with ExitStack() as ctx:
        const = ctx.enter_context(tc.tile_pool(name="const", bufs=1))
        ts_pool = ctx.enter_context(tc.tile_pool(name="ts", bufs=4))
        work = ctx.enter_context(tc.tile_pool(name="work", bufs=2))
        stage = ctx.enter_context(tc.tile_pool(name="stage", bufs=8))
        ps_a = ctx.enter_context(tc.psum_pool(name="ps_a", bufs=2))
        ps_o = ctx.enter_context(tc.psum_pool(name="ps_o", bufs=4))
        ctx.enter_context(tc.manual_schedule())

        x0 = const.tile([P, 24, n_feat], BF16)
        x2 = const.tile([P, 21, n_feat], BF16)
        xz = const.tile([P, 10, n_feat], BF16)
        xf = const.tile([P, 2, n_feat], BF16)
        w_raw = const.tile([P, n_t, n_out], BF16)
        b_bc = const.tile([P, n_out], BF16)
        id32 = const.tile([P, P], F32)
        idx = const.tile([P, 32], F32, align_bytes=64)
        low = const.tile([P, 32], F32, align_bytes=64)
        dif = const.tile([P, 32], F32)
        sq = const.tile([P, 32], F32)
        pat = const.tile([P, 96], BF16)
        blk = const.tile([P, 32], F32)
        adj = const.tile([P, 192], BF16)
        cyc_up = const.tile([P, P], F32)
        cyc_dn = const.tile([P, P], F32)
        w_grp = const.tile([P, n_out, n_t], BF16, align_bytes=64)
        w_q = const.tile([P, n_out], U32, align_bytes=64)
        w_s = const.tile([P, n_out], U8, align_bytes=64)
        bias = const.tile([P, n_out], F32)
        fix = const.tile([P, 8, 2, 4, n_t], BF16)

        def load_x0(img, lo, hi):
            nc.sync.dma_start(out=x0[:, 8 * img + lo:8 * img + hi, :],
                              in_=X[img, P * lo:P * hi, :].rearrange("(j p) f -> p j f", p=P))

        def load_x2(img, lo, hi):
            nc.sync.dma_start(out=x2[:, 7 * img + lo:7 * img + hi, :],
                              in_=X[img, 64 + P * lo:64 + P * hi, :].rearrange("(j p) f -> p j f", p=P))

        nc.vector.memset(xz[:, 0, :], 0.0)
        nc.vector.memset(xz[:, 9, :], 0.0)
        load_x0(0, 0, 2)
        load_x2(0, 0, 2)
        nc.sync.dma_start(out=w_raw[:, :, 0:512], in_=w_view[:, :, 0:512])
        nc.sync.dma_start(out=w_raw[:, :, 512:1024], in_=w_view[:, :, 512:1024])
        nc.scalar.dma_start(out=b_bc[:], in_=b.partition_broadcast(P))
        load_x0(0, 2, 4)
        load_x2(0, 2, 4)
        load_x0(0, 4, 8)
        load_x2(0, 4, 7)
        nc.sync.dma_start(out=xz[:, 1:5, :], in_=xz_view[:, 0:4, :])
        for cq in range(1, 4):
            nc.sync.dma_start(out=xz[cq:128:4, 0, :], in_=xz_rows[:, 8 * cq - 1, :])
        nc.sync.dma_start(out=xf[:, 0, :], in_=X[z_img, 0:128, :])
        nc.sync.dma_start(out=xf[:, 1, :], in_=X[z_img, 896:1024, :])
        load_x0(1, 0, 4)
        load_x2(1, 0, 4)
        nc.sync.dma_start(out=xz[:, 5:9, :], in_=xz_view[:, 4:8, :])
        for cq in range(0, 3):
            nc.sync.dma_start(out=xz[cq:128:4, 9, :], in_=xz_rows[:, 8 * cq + 8, :])

        later_loads = {0: (1, 1), 2: (2, 0), 5: (2, 1)}

        def load_half_image(img, half):
            load_x0(img, 4 * half, 4 * half + 4)
            load_x2(img, 4 * half, min(4 * half + 4, 7))

        nc.vector.memset(adj[:], 0.0)
        nc.vector.memset(id32[:], 0.0)
        nc.vector.memset(idx[:, 0:1], 0.0)
        for w in (1, 2, 4, 8, 16):
            nc.vector.tensor_scalar_add(out=idx[:, w:2 * w], in0=idx[:, 0:w], scalar1=float(w))
        nc.vector.transpose(out=low[:], in_=idx[:])
        nc.vector.tensor_scalar(out=dif[:], in0=idx[:], scalar1=low[:, 0:1], scalar2=None,
                                op0=mybir.AluOpType.subtract)
        nc.vector.tensor_tensor(out=sq[:], in0=dif[:], in1=dif[:], op=mybir.AluOpType.mult)
        nc.vector.tensor_scalar(out=pat[:, 0:32], in0=sq[:], scalar1=1.0, scalar2=None, op0=mybir.AluOpType.is_le)
        nc.vector.tensor_scalar(out=pat[:, 32:64], in0=sq[:], scalar1=1.0, scalar2=None, op0=mybir.AluOpType.is_equal)
        nc.vector.tensor_scalar(out=pat[:, 64:96], in0=sq[:], scalar1=1.0, scalar2=None, op0=mybir.AluOpType.is_le)
        for rl in range(4):
            rows = slice(32 * rl, 32 * rl + 32)
            nc.vector.tensor_copy(out=adj[rows, 32 * rl:32 * rl + 96], in_=pat[rows, :])

        def regroup(copy, lo, hi):
            copy(out=w_grp[:, lo:hi, :], in_=w_raw[:, :, lo:hi].rearrange("p t n -> p n t"))

        def weights_q(h):
            cols = slice(512 * h, 512 * h + 512)
            nc.vector.quantize_mx(out=w_q[:, cols].bitcast(FP8X4), scales=w_s[:, cols],
                                  in_=w_grp[:, cols, :].rearrange("p n t -> p (n t)"))

        def shifts():
            nc.vector.tensor_scalar(out=blk[:], in0=sq[:], scalar1=0.0, scalar2=None, op0=mybir.AluOpType.is_equal)
            for q in range(4):
                rows = slice(32 * q, 32 * q + 32)
                nc.vector.tensor_copy(out=id32[rows, 32 * q:32 * q + 32], in_=blk[rows, :])
            nc.vector.tensor_copy(out=cyc_up[:, 4:128], in_=id32[:, 0:124])
            nc.vector.tensor_copy(out=cyc_up[:, 0:4], in_=id32[:, 124:128])
            nc.vector.tensor_copy(out=cyc_dn[:, 0:124], in_=id32[:, 4:128])
            nc.vector.tensor_copy(out=cyc_dn[:, 124:128], in_=id32[:, 0:4])

        def border_rows_sum():
            acc_f = ps_a.tile([P, n_t, P], F32, tag="acc1")
            for t in range(n_t):
                f = slice(P * t, P * t + P)
                nc.tensor.matmul(acc_f[:, t, 0:32], lhsT=xf[:, 0, f], rhs=adj[:, 32:64], start=True, stop=True)
                nc.tensor.matmul(acc_f[:, t, 32:64], lhsT=xf[:, 1, f], rhs=adj[:, 128:160], start=True, stop=True)
            return acc_f

        def border_rows_round(acc_f):
            for rr in range(2):
                nc.scalar.copy(out=fix[:, :, rr, :, :],
                               in_=acc_f[:, :, 32 * rr:32 * rr + 32].rearrange("p t (q i) -> p i q t", q=4))

        def row_sums(ci):
            t32 = ts_pool.tile([P, n_feat], F32, tag="t32")
            s32 = ts_pool.tile([P, n_feat], F32, tag="s32")
            nc.vector.tensor_tensor(out=t32[:], in0=xz[:, ci, :], in1=xz[:, ci + 2, :], op=ADD)
            nc.vector.tensor_tensor(out=s32[:], in0=t32[:], in1=xz[:, ci + 1, :], op=ADD)
            return t32, s32

        def z_sum(acc, t32, s32):
            for t in range(n_t):
                f = slice(P * t, P * t + P)
                nc.tensor.matmul(acc[:, t, :], lhsT=t32[:, f], rhs=id32[:], is_transpose=True, start=True, stop=False)
                nc.tensor.matmul(acc[:, t, :], lhsT=s32[:, f], rhs=cyc_up[:], is_transpose=True, start=False, stop=False)
                nc.tensor.matmul(acc[:, t, :], lhsT=s32[:, f], rhs=cyc_dn[:], is_transpose=True, start=False, stop=True)

        def p_parts(n):
            img = n // 8
            u = n % 8
            if u < 7:
                return [(x0, 8 * img + u, 64, 0, 64), (x2, 7 * img + u, 64, 64, 64)]
            return [(x0, 8 * img, 32, 0, 32), (x0, 8 * img + 7, 64, 32, 64), (x0, 8 * img + 7, 128, 96, 32)]

        def p_sum(acc, n):
            for t in range(n_t):
                f = slice(P * t, P * t + P)
                for (src, blk, a_lo, o_lo, width) in p_parts(n):
                    nc.tensor.matmul(acc[:, t, o_lo:o_lo + width], lhsT=src[:, blk, f], rhs=adj[:, a_lo:a_lo + width],
                                     start=True, stop=True)

        def p_stores(n):
            img = n // 8
            u = n % 8
            if u < 7:
                return [(0, P, out[img, P * u + 32:P * u + 160, :])]
            return [(0, 32, out[img, 0:32, :]), (32, 96, out[img, 928:992, :]), (96, P, out[img, 992:1024, :])]

        pairs = []
        first_use = {}
        n_p = 0
        n_z = 0
        for s, kind in enumerate(PAIR_KINDS):
            if kind == "A":
                pairs.append([("p", n_p), ("p", n_p + 1)])
                n_p += 2
            else:
                pairs.append([("p", n_p), ("z", n_z)])
                first_use[s] = n_z
                n_p += 1
                n_z += 1

        def pair_tiles(s):
            return pairs[s]

        def neighbour_sums(s, sums):
            accs = []
            for a, (kind, n) in enumerate(pair_tiles(s)):
                acc = ps_a.tile([P, n_t, P], F32, tag="acc%d" % a, name="acc%d" % a)
                if kind == "p":
                    p_sum(acc, n)
                else:
                    z_sum(acc, sums[n][0], sums[n][1])
                accs.append(acc)
            return accs

        def round_out(s, a, accs, grp):
            kind, n = pair_tiles(s)[a]
            nc.scalar.copy(out=grp[:, a, :, :], in_=accs[a][:].rearrange("p t n -> p n t"))
            if kind == "z":
                nc.scalar.copy(out=grp[:, a, 0:4, :], in_=fix[:, n, 0, :, :])
                nc.scalar.copy(out=grp[:, a, 124:128, :], in_=fix[:, n, 1, :, :])

        def quantise(grp):
            a_q = work.tile([P, 2 * P], U32, align_bytes=64, tag="a_q")
            a_s = work.tile([P, 2 * P], U8, align_bytes=64, tag="a_s")
            nc.vector.quantize_mx(out=a_q[:].bitcast(FP8X4), scales=a_s[:],
                                  in_=grp[:].rearrange("p a n t -> p (a n t)"))
            return a_q, a_s

        def multiply(a_q, a_s):
            banks = []
            for h in range(2):
                cols = slice(512 * h, 512 * h + 512)
                for a in range(2):
                    nodes = slice(P * a, P * a + P)
                    po = ps_o.tile([P, 512], F32, tag="po", name="po%d%d" % (h, a))
                    nc.tensor.matmul_mx(out=po[:], lhsT=a_q[:, nodes].bitcast(FP8X4), lhsT_scale=a_s[:, nodes],
                                        rhs=w_q[:, cols].bitcast(FP8X4), rhs_scale=w_s[:, cols],
                                        start=True, stop=True)
                    banks.append(po)
            return banks

        def out_tiles():
            o_tiles = []
            for a in range(2):
                o_new = stage.tile([P, n_out], F32, tag="o_sb", name="o_sb%d" % a)
                o_tiles.append(o_new)
            return o_tiles

        def add_bias(k, banks, o_tiles):
            cols = slice(512 * (k // 2), 512 * (k // 2) + 512)
            o_sb = o_tiles[k % 2]
            if k in G_HALVES:
                nc.scalar.copy(out=o_sb[:, cols], in_=banks[k][:])
                nc.gpsimd.tensor_tensor(out=o_sb[:, cols], in0=o_sb[:, cols], in1=bias[:, cols], op=ADD)
            else:
                nc.vector.tensor_tensor(out=o_sb[:, cols], in0=banks[k][:], in1=bias[:, cols], op=ADD)

        def store(s, a, o_tiles):
            kind, n = pair_tiles(s)[a]
            if kind == "z":
                nc.sync.dma_start(out=oz_view[:, n, :], in_=o_tiles[a][:])
            else:
                for (lo, hi, dest) in p_stores(n):
                    nc.sync.dma_start(out=dest, in_=o_tiles[a][lo:hi, :])

        n_pairs = len(PAIR_KINDS)
        sums = {}
        shifts()
        regroup(nc.vector.tensor_copy, 0, 512)
        weights_q(0)
        accs = neighbour_sums(0, sums)
        grp_next = work.tile([P, 2, P, n_t], BF16, align_bytes=64, tag="grp")
        round_out(0, 0, accs, grp_next)
        round_out(0, 1, accs, grp_next)
        regroup(nc.scalar.copy, 768, 1024)
        nc.scalar.copy(out=bias[:], in_=b_bc[:])
        regroup(nc.vector.tensor_copy, 512, 768)
        ready = quantise(grp_next)
        weights_q(1)
        sums_after = {}
        for s in sorted(first_use):
            sums_after[max(s - 4, 0)] = first_use[s]
        for s in range(n_pairs):
            more = s + 1 < n_pairs
            if more:
                accs = neighbour_sums(s + 1, sums)
            banks = multiply(ready[0], ready[1])
            if s == 1:
                acc_f = border_rows_sum()
            o_tiles = out_tiles()
            if more:
                grp_next = work.tile([P, 2, P, n_t], BF16, align_bytes=64, tag="grp")
                round_out(s + 1, 0, accs, grp_next)
                round_out(s + 1, 1, accs, grp_next)
                ready = quantise(grp_next)
            add_bias(0, banks, o_tiles)
            if s == 1:
                border_rows_round(acc_f)
            add_bias(1, banks, o_tiles)
            add_bias(2, banks, o_tiles)
            store(s, 0, o_tiles)
            add_bias(3, banks, o_tiles)
            store(s, 1, o_tiles)
            if s in later_loads:
                load_half_image(later_loads[s][0], later_loads[s][1])
            if s in sums_after:
                sums[sums_after[s]] = row_sums(sums_after[s])
